import numpy as np
import ml_dtypes


def mxq(x, axis, fmt="e4m3"):
    dtype, down = {"e4m3": (ml_dtypes.float8_e4m3fn, 7), "e5m2": (ml_dtypes.float8_e5m2, 14)}[fmt]
    v = np.moveaxis(np.asarray(x, np.float32).astype(ml_dtypes.bfloat16).astype(np.float64), axis, -1)
    blocks = v.reshape(v.shape[:-1] + (-1, 32))
    amax = np.abs(blocks).max(-1, keepdims=True)
    byte = np.maximum(np.where(amax > 0, np.frexp(amax)[1] - 1 + 127, 0) - down, 1)
    scale = np.exp2(byte - 127.0)
    codes = (blocks / scale).astype(np.float32).astype(dtype).astype(np.float64)
    return np.moveaxis((codes * scale).reshape(v.shape), -1, axis)


WIDE = False


def mx_kscale(k):
    if not WIDE:
        return np.ones(k)
    levels = np.array([10, -10, 5, -5, 0])
    if k % 512:
        return np.exp2(np.random.permutation(np.resize(levels, k // 32))).repeat(32)
    a = np.empty((k // 512, 16))
    for p in range(k // 512):
        a[p, :8] = np.random.permutation(np.resize(levels, 8))
        for g in range(8):
            far = levels[np.abs(levels - a[p, g]) >= 10]
            a[p, g + 8] = far[np.random.randint(len(far))]
    return np.exp2(a.ravel()).repeat(32)


BF16 = ml_dtypes.bfloat16


def bf(x):
    return np.asarray(x, np.float32).astype(BF16)


def f64(x):
    return np.asarray(x).astype(np.float64)


T, D, E, BLK = 8192, 1024, 128, 512
EPS = 1e-05


def setup_inputs():
    s = mx_kscale(D)
    rs = 10.0 ** np.random.uniform(-2.5, 0.5, (T, 1))
    return {"h": bf((np.random.standard_normal((T, D)) + 0.3) * rs),
            "ln_w": bf(np.random.standard_normal(D) * s),
            "ln_b": bf(np.random.standard_normal(D) * 0.3 * s),
            "w_q": bf(np.random.standard_normal((E, D)) * 1.6 / np.sqrt(D) / s),
            "w_k": bf(np.random.standard_normal((E, D)) * 1.6 / np.sqrt(D) / s),
            "w_v": bf(np.random.standard_normal((E, D)) * 1.0 / np.sqrt(D) / s)}


def reference(h, ln_w, ln_b, w_q, w_k, w_v):
    h = f64(h)
    mu = h.mean(-1, keepdims=True)
    var = np.square(h - mu).mean(-1, keepdims=True)
    h_norm = (h - mu) / np.sqrt(var + EPS) * f64(ln_w) + f64(ln_b)
    hq = mxq(h_norm, 1, "e4m3")
    q = hq @ mxq(f64(w_q), 1, "e4m3").T
    k = hq @ mxq(f64(w_k), 1, "e4m3").T
    v = hq @ mxq(f64(w_v), 1, "e4m3").T
    return q, k, v

@@ -1,0 +1,339 @@
+from contextlib import ExitStack
+
+import concourse.mybir as mybir
+from concourse.masks import make_identity
+
+F32 = mybir.dt.float32
+BF16 = mybir.dt.bfloat16
+U32 = mybir.dt.uint32
+U8 = mybir.dt.uint8
+FP8X4 = mybir.dt.float8_e4m3fn_x4
+ALU = mybir.AluOpType
+ACT = mybir.ActivationFunctionType
+
+T, D, E = 8192, 1024, 128
+EPS = 1e-05
+FLOPS = 2 * T * D * 3 * E
+
+P = 128
+NT = T // P
+GT = 4
+NG = NT // GT
+GTOK = GT * P
+KP = 512
+NC = D // KP
+NU = NG * NC
+HBUFS = 8
+
+A0 = 7
+VE = 5
+SQ = 4
+RC = 3
+BV = 3
+BS = 1
+ML = 2
+
+
+def n_scalar_norm(g):
+    if g < 3:
+        return 4
+    if g >= 12:
+        return min(2, NG - 1 - g)
+    return 3 if g % 2 == 1 else 2
+
+
+def n_vector_out(g):
+    if g < 11:
+        return 0
+    return 2 if g in (13, 15) else 1
+
+
+def n_vector_leave(u):
+    return 1 if u == NU - 1 else 0
+
+
+def group_of(t, lead):
+    g, r = divmod(t + lead, 2)
+    return g if r == 0 and 0 <= g < NG else None
+
+
+def tile_toyattnsublayer_pa_t_kernel(tc, h, ln_w, ln_b, w_q, w_k, w_v, out_0, out_1, out_2):
+    nc = tc.nc
+    h_v = h.rearrange("(p n) k -> p n k", n=NT)
+    outs_v = [o.rearrange("(p n) e -> p n e", n=NT) for o in (out_0, out_1, out_2)]
+
+    with ExitStack() as ctx:
+        const = ctx.enter_context(tc.tile_pool(name="const", bufs=1))
+        hpool = ctx.enter_context(tc.tile_pool(name="hpool", bufs=HBUFS))
+        small = ctx.enter_context(tc.tile_pool(name="small", bufs=4))
+        xpool = ctx.enter_context(tc.tile_pool(name="xpool", bufs=2))
+        plpool = ctx.enter_context(tc.tile_pool(name="plpool", bufs=3))
+        grpool = ctx.enter_context(tc.tile_pool(name="grpool", bufs=3))
+        cpool = ctx.enter_context(tc.tile_pool(name="cpool", bufs=4))
+        opool = ctx.enter_context(tc.tile_pool(name="opool", bufs=3))
+        psum = ctx.enter_context(tc.psum_pool(name="psum", bufs=1))
+        ctx.enter_context(tc.manual_schedule())
+
+        hts, sts, mvs, rstds, nmrs, xhs = {}, {}, {}, {}, {}, {}
+        vepss, stds = {}, {}
+        tps, pls, grs, cds, scs, accs, osts = {}, {}, {}, {}, {}, {}, {}
+
+        def load(g, tiles=None):
+            if g not in hts:
+                hts[g] = hpool.tile([P, GT, D], BF16, name="ht")
+            ht = hts[g]
+            if tiles is None:
+                nc.sync.dma_start(out=ht[:], in_=h_v[:, GT * g : GT * (g + 1), :])
+            else:
+                for i in tiles:
+                    n = 2 if i == 0 else 1
+                    for a in range(n):
+                        cols = slice(D // n * a, D // n * (a + 1))
+                        nc.sync.dma_start(out=ht[:, i, cols], in_=h_v[:, GT * g + i, cols])
+
+        def stats(g, pairs):
+            if g not in sts:
+                sts[g] = small.tile([P, GT, 2, 6], F32, name="st")
+            for i, a in pairs:
+                nc.vector.bn_stats(out=sts[g][:, i, a, :], in_=hts[g][:, i, 512 * a : 512 * (a + 1)])
+
+        def aggregate(g):
+            mvs[g] = small.tile([P, GT, 2], F32, name="mv")
+            for i in range(GT):
+                nc.vector.bn_aggr(out=mvs[g][:, i, :], in_=sts[g][:, i, :, :].rearrange("p a b -> p (a b)"))
+
+        def add_eps(g):
+            vepss[g] = small.tile([P, GT], F32, name="veps")
+            nc.vector.tensor_scalar(out=vepss[g][:], in0=mvs[g][:, :, 1], scalar1=EPS, scalar2=None, op0=ALU.add)
+
+        def root(g):
+            stds[g] = small.tile([P, GT], F32, name="std")
+            nc.scalar.activation(out=stds[g][:], in_=vepss[g][:], func=ACT.Sqrt)
+
+        def reciprocal(g):
+            rstds[g] = small.tile([P, GT], F32, name="rstd")
+            nc.vector.reciprocal(rstds[g][:], stds[g][:])
+
+        def neg_mean_rstd(g):
+            nmrs[g] = small.tile([P, GT], F32, name="nmr")
+            nc.vector.scalar_tensor_tensor(
+                out=nmrs[g][:], in0=mvs[g][:, :, 0], scalar=-1.0, in1=rstds[g][:], op0=ALU.mult, op1=ALU.mult
+            )
+
+        def normalise(g, i, on_vector):
+            if g not in xhs:
+                xhs[g] = xpool.tile([P, GT, 4, D // 4], F32, name="xh")
+            src = hts[g][:, i, :].rearrange("p (b j r) -> p j b r", j=4, r=8)
+            dst = xhs[g][:, i, :, :].rearrange("p j (b r) -> p j b r", r=8)
+            if on_vector:
+                nc.vector.tensor_scalar(
+                    out=dst,
+                    in0=src,
+                    scalar1=mvs[g][:, i, 0:1],
+                    scalar2=rstds[g][:, i : i + 1],
+                    op0=ALU.subtract,
+                    op1=ALU.mult,
+                )
+            else:
+                nc.scalar.activation(
+                    out=dst,
+                    in_=src,
+                    func=ACT.Identity,
+                    scale=rstds[g][:, i : i + 1],
+                    bias=nmrs[g][:, i : i + 1],
+                )
+
+        def transposes(u, j):
+            g, c = divmod(u, NC)
+            tp = psum.tile([P, GTOK], F32, name="tp", tag="T%d" % j)
+            tps[(u, j)] = tp
+            for i in range(GT):
+                nc.tensor.transpose(tp[:, P * i : P * (i + 1)], xhs[g][:, i, j, P * c : P * (c + 1)], ident_f[:])
+
+        def leave(u, j, on_vector):
+            kb = 4 * (u % NC) + j
+            if u not in pls:
+                pls[u] = plpool.tile([P, 4, GTOK], BF16, name="pl")
+            if on_vector:
+                nc.vector.tensor_scalar(
+                    out=pls[u][:, j, :],
+                    in0=tps[(u, j)][:],
+                    scalar1=wb[:, kb : kb + 1],
+                    scalar2=wb[:, 8 + kb : 9 + kb],
+                    op0=ALU.mult,
+                    op1=ALU.add,
+                )
+            else:
+                nc.scalar.activation(
+                    out=pls[u][:, j, :],
+                    in_=tps[(u, j)][:],
+                    func=ACT.Identity,
+                    scale=wb[:, kb : kb + 1],
+                    bias=wb[:, 8 + kb : 9 + kb],
+                )
+
+        def pieces(u):
+            n = 2 if u == NU - 1 else 1
+            return [slice(GTOK // n * a, GTOK // n * (a + 1)) for a in range(n)]
+
+        def regroup(u):
+            grs[u] = grpool.tile([P, GTOK, 4], BF16, name="gr", align_bytes=64)
+            for tok in pieces(u):
+                nc.vector.tensor_copy(
+                    out=grs[u][:, tok, :].rearrange("p (c i) t -> p c t i", i=4),
+                    in_=pls[u][:, :, tok].rearrange("p t (c i) -> p c t i", i=4),
+                )
+
+        def quantise(u):
+            cds[u] = cpool.tile([P, GTOK], U32, name="codes", align_bytes=64)
+            scs[u] = cpool.tile([P, GTOK], U8, name="scl", align_bytes=64)
+            for tok in pieces(u):
+                nc.vector.quantize_mx(
+                    out=cds[u][:, tok].bitcast(FP8X4),
+                    scales=scs[u][:, tok],
+                    in_=grs[u][:, tok, :].rearrange("p n j -> p (n j)"),
+                )
+
+        def multiply(u):
+            g, c = divmod(u, NC)
+            if c == 0:
+                accs[g] = [psum.tile([P, 512], F32, name="acc%d" % i, tag="O%d" % i) for i in range(GT)]
+            for i in range(GT):
+                nc.tensor.matmul_mx(
+                    out=accs[g][i][:],
+                    lhsT=cds[u][:, P * i : P * (i + 1)].bitcast(FP8X4),
+                    lhsT_scale=scs[u][:, P * i : P * (i + 1)],
+                    rhs=wcodes[:, c, :].bitcast(FP8X4),
+                    rhs_scale=wscales[:, c, :],
+                    start=(c == 0),
+                    stop=(c == NC - 1),
+                )
+
+        def out_copy(g, i, on_vector):
+            if g not in osts:
+                osts[g] = opool.tile([P, 3, GT, E], F32, name="ost")
+            src = accs[g][i][:, 0 : 3 * E].rearrange("p (s e) -> p s e", s=3)
+            if on_vector:
+                nc.vector.tensor_copy(out=osts[g][:, :, i, :], in_=src)
+            else:
+                nc.scalar.copy(out=osts[g][:, :, i, :], in_=src)
+
+        def store(g):
+            for s in range(3):
+                nc.sync.dma_start(out=outs_v[s][:, GT * g : GT * (g + 1), :], in_=osts[g][:, s, :, :])
+
+        ident_b = const.tile([P, P], BF16, name="ident_b")
+        make_identity(nc, ident_b[:])
+        ident_f = const.tile([P, P], F32, name="ident_f")
+        make_identity(nc, ident_f[:])
+        lnrows = const.tile([P, P], BF16, name="lnrows")
+        nc.vector.memset(lnrows[:], 0.0)
+        wg = const.tile([P, NC, 512, 4], BF16, name="wg", align_bytes=64)
+        nc.vector.memset(wg[:, :, 3 * E : 512, :], 0.0)
+
+        load(0, (0, 1))
+        for r, vec in enumerate((ln_w, ln_b)):
+            for c in range(NC):
+                nc.sync.dma_start(
+                    out=lnrows[8 * r + 4 * c : 8 * r + 4 * (c + 1), :].rearrange("j (b r) -> j b r", r=8),
+                    in_=vec[KP * c : KP * (c + 1)].rearrange("(b j r) -> j b r", j=4, r=8),
+                )
+        load(0, (2, 3))
+        load(1)
+        wraw = const.tile([P, 3, D], BF16, name="wraw")
+        for s, w in enumerate((w_q, w_k, w_v)):
+            nc.sync.dma_start(out=wraw[:, s, :], in_=w)
+        for g in range(2, HBUFS):
+            load(g)
+        wslots = const.tile([P, 3, 4, D // 4], BF16, name="wslots")
+
+        ln_ps = psum.tile([P, P], BF16, name="ln_ps", tag="O2")
+        nc.tensor.transpose(ln_ps[:], lnrows[:], ident_b[:])
+        wb = const.tile([P, 16], F32, name="wb")
+        nc.scalar.copy(out=wb[:], in_=ln_ps[:, 0:16])
+        for s in range(3):
+            nc.scalar.copy(
+                out=wslots[:, s, :, :].rearrange("p j (b r) -> p j b r", r=8),
+                in_=wraw[:, s, :].rearrange("p (b j r) -> p j b r", j=4, r=8),
+            )
+        wtags = ("T0", "T1", "T2", "T3", "O0", "O1")
+        for c in range(NC):
+            for s in range(3):
+                wt = psum.tile([P, 4, E], BF16, name="wt", tag=wtags[3 * c + s])
+                for j in range(4):
+                    nc.tensor.transpose(wt[:, j, :], wslots[:, s, j, P * c : P * (c + 1)], ident_b[:])
+                nc.scalar.copy(out=wg[:, c, E * s : E * (s + 1), :], in_=wt[:].rearrange("p j e -> p e j"))
+        wcodes = const.tile([P, NC, 512], U32, name="wcodes", align_bytes=64)
+        wscales = const.tile([P, NC, 512], U8, name="wscales", align_bytes=64)
+
+        for t in range(-A0, NU + ML + 1):
+            in_u = 0 <= t < NU
+            prev_u = 0 <= t - 1 < NU
+            g_bs = group_of(t, BS)
+            g_bv = group_of(t, BV)
+            g_f = group_of(t, -(ML + 2))
+            g_ve = group_of(t, VE)
+            g_sq = group_of(t, SQ)
+            g_rc = group_of(t, RC)
+            g_s, second = divmod(t + A0, 2)
+            have_s = 0 <= g_s < NG
+            pairs = [(2 * second + i, a) for i in range(2) for a in range(2)]
+            n_fs = GT - n_vector_out(g_f) if g_f is not None else 0
+
+            if g_sq is not None:
+                root(g_sq)
+            if g_bs is not None:
+                for i in range(n_scalar_norm(g_bs)):
+                    normalise(g_bs, GT - 1 - i, False)
+                if g_bs + HBUFS < NG:
+                    load(g_bs + HBUFS)
+            if prev_u:
+                regroup(t - 1)
+            for j in range(2):
+                if in_u:
+                    leave(t, j, False)
+                if -1 <= t < NU - 1:
+                    transposes(t + 1, j)
+            if g_f is not None:
+                for i in range(GT):
+                    out_copy(g_f, i, i >= n_fs)
+                store(g_f)
+            if 0 <= t - ML < NU:
+                multiply(t - ML)
+            if g_ve is not None:
+                add_eps(g_ve)
+            if g_rc is not None:
+                reciprocal(g_rc)
+            if have_s:
+                stats(g_s, pairs[0:2])
+            if t == -2:
+                nc.vector.quantize_mx(
+                    out=wcodes[:].rearrange("p c n -> p (c n)").bitcast(FP8X4),
+                    scales=wscales[:].rearrange("p c n -> p (c n)"),
+                    in_=wg[:].rearrange("p c n j -> p (c n j)"),
+                )
+            n_vl = n_vector_leave(t) if in_u else 0
+            if not have_s:
+                if g_bv is not None:
+                    for i in range(GT - n_scalar_norm(g_bv)):
+                        normalise(g_bv, i, True)
+                for j in range(4 - n_vl, 4):
+                    leave(t, j, True)
+                    if t < NU - 1:
+                        transposes(t + 1, j)
+            if prev_u:
+                quantise(t - 1)
+            if g_rc is not None:
+                neg_mean_rstd(g_rc)
+            for j in range(2, 4 - n_vl):
+                if in_u:
+                    leave(t, j, False)
+                if -1 <= t < NU - 1:
+                    transposes(t + 1, j)
+            if have_s:
+                stats(g_s, pairs[2:4])
+                if g_bv is not None:
+                    for i in range(GT - n_scalar_norm(g_bv)):
+                        normalise(g_bv, i, True)
+            if have_s and second == 1:
+                aggregate(g_s)

@@ -25,36 +25,26 @@ NC = D // KP
 NU = NG * NC
 HBUFS = 8
 
-A0 = 7
-VE = 5
-SQ = 4
-RC = 3
-BV = 3
-BS = 1
+ST = 4
+NM = 3
 ML = 2
 
 
-def n_scalar_norm(g):
-    if g < 3:
-        return 4
-    if g >= 12:
-        return min(2, NG - 1 - g)
-    return 3 if g % 2 == 1 else 2
+def on_scalar(g, i):
+    if g == 0:
+        return True
+    if g == 1:
+        return i < 2
+    return i == 0
 
 
-def n_vector_out(g):
-    if g < 11:
-        return 0
-    return 2 if g in (13, 15) else 1
+def vector_out(g):
+    return 2 * g + ML + 2 >= 2 * NG - ST + 2
 
 
-def n_vector_leave(u):
-    return 1 if u == NU - 1 else 0
-
-
-def group_of(t, lead):
+def half_of(t, lead):
     g, r = divmod(t + lead, 2)
-    return g if r == 0 and 0 <= g < NG else None
+    return (g, (2 * r, 2 * r + 1)) if 0 <= g < NG else None
 
 
 def tile_toyattnsublayer_pa_t_kernel(tc, h, ln_w, ln_b, w_q, w_k, w_v, out_0, out_1, out_2):
@@ -66,7 +56,7 @@ def tile_toyattnsublayer_pa_t_kernel(tc, h, ln_w, ln_b, w_q, w_k, w_v, out_0, ou
         const = ctx.enter_context(tc.tile_pool(name="const", bufs=1))
         hpool = ctx.enter_context(tc.tile_pool(name="hpool", bufs=HBUFS))
         small = ctx.enter_context(tc.tile_pool(name="small", bufs=4))
-        xpool = ctx.enter_context(tc.tile_pool(name="xpool", bufs=2))
+        xpool = ctx.enter_context(tc.tile_pool(name="xpool", bufs=3))
         plpool = ctx.enter_context(tc.tile_pool(name="plpool", bufs=3))
         grpool = ctx.enter_context(tc.tile_pool(name="grpool", bufs=3))
         cpool = ctx.enter_context(tc.tile_pool(name="cpool", bufs=4))
@@ -74,8 +64,7 @@ def tile_toyattnsublayer_pa_t_kernel(tc, h, ln_w, ln_b, w_q, w_k, w_v, out_0, ou
         psum = ctx.enter_context(tc.psum_pool(name="psum", bufs=1))
         ctx.enter_context(tc.manual_schedule())
 
-        hts, sts, mvs, rstds, nmrs, xhs = {}, {}, {}, {}, {}, {}
-        vepss, stds = {}, {}
+        hts, sts, mvs, stds, rstds, nmrs, xhs = {}, {}, {}, {}, {}, {}, {}
         tps, pls, grs, cds, scs, accs, osts = {}, {}, {}, {}, {}, {}, {}
 
         def load(g, tiles=None):
@@ -86,61 +75,68 @@ def tile_toyattnsublayer_pa_t_kernel(tc, h, ln_w, ln_b, w_q, w_k, w_v, out_0, ou
                 nc.sync.dma_start(out=ht[:], in_=h_v[:, GT * g : GT * (g + 1), :])
             else:
                 for i in tiles:
-                    n = 2 if i == 0 else 1
+                    n = 2 if (g, i) == (0, 0) else 1
                     for a in range(n):
                         cols = slice(D // n * a, D // n * (a + 1))
                         nc.sync.dma_start(out=ht[:, i, cols], in_=h_v[:, GT * g + i, cols])
 
-        def stats(g, pairs):
+        def stats(g, i):
             if g not in sts:
                 sts[g] = small.tile([P, GT, 2, 6], F32, name="st")
-            for i, a in pairs:
+            for a in range(2):
                 nc.vector.bn_stats(out=sts[g][:, i, a, :], in_=hts[g][:, i, 512 * a : 512 * (a + 1)])
 
-        def aggregate(g):
-            mvs[g] = small.tile([P, GT, 2], F32, name="mv")
-            for i in range(GT):
-                nc.vector.bn_aggr(out=mvs[g][:, i, :], in_=sts[g][:, i, :, :].rearrange("p a b -> p (a b)"))
+        def aggregate(g, i):
+            if g not in mvs:
+                mvs[g] = small.tile([P, GT, 2], F32, name="mv")
+            nc.vector.bn_aggr(out=mvs[g][:, i, :], in_=sts[g][:, i, :, :].rearrange("p a b -> p (a b)"))
 
-        def add_eps(g):
-            vepss[g] = small.tile([P, GT], F32, name="veps")
-            nc.vector.tensor_scalar(out=vepss[g][:], in0=mvs[g][:, :, 1], scalar1=EPS, scalar2=None, op0=ALU.add)
+        def root(g, tiles):
+            if g not in stds:
+                stds[g] = small.tile([P, GT], F32, name="std")
+            cols = slice(tiles[0], tiles[-1] + 1)
+            nc.scalar.activation(out=stds[g][:, cols], in_=mvs[g][:, cols, 1], func=ACT.Sqrt, bias=eps_t[:])
 
-        def root(g):
-            stds[g] = small.tile([P, GT], F32, name="std")
-            nc.scalar.activation(out=stds[g][:], in_=vepss[g][:], func=ACT.Sqrt)
+        def reciprocal(g, tiles):
+            if g not in rstds:
+                rstds[g] = small.tile([P, GT], F32, name="rstd")
+            cols = slice(tiles[0], tiles[-1] + 1)
+            nc.vector.reciprocal(rstds[g][:, cols], stds[g][:, cols])
 
-        def reciprocal(g):
-            rstds[g] = small.tile([P, GT], F32, name="rstd")
-            nc.vector.reciprocal(rstds[g][:], stds[g][:])
-
-        def neg_mean_rstd(g):
-            nmrs[g] = small.tile([P, GT], F32, name="nmr")
-            nc.vector.scalar_tensor_tensor(
-                out=nmrs[g][:], in0=mvs[g][:, :, 0], scalar=-1.0, in1=rstds[g][:], op0=ALU.mult, op1=ALU.mult
+        def neg_mean_rstd(g, i):
+            if g not in nmrs:
+                nmrs[g] = small.tile([P, GT], F32, name="nmr")
+            eng = nc.vector if g == 0 else nc.gpsimd
+            eng.tensor_scalar(
+                out=nmrs[g][:, i : i + 1],
+                in0=mvs[g][:, i, 0:1],
+                scalar1=rstds[g][:, i : i + 1],
+                scalar2=-1.0,
+                op0=ALU.mult,
+                op1=ALU.mult,
             )
 
-        def normalise(g, i, on_vector):
+        def normalise(g, i):
             if g not in xhs:
                 xhs[g] = xpool.tile([P, GT, 4, D // 4], F32, name="xh")
             src = hts[g][:, i, :].rearrange("p (b j r) -> p j b r", j=4, r=8)
             dst = xhs[g][:, i, :, :].rearrange("p j (b r) -> p j b r", r=8)
-            if on_vector:
-                nc.vector.tensor_scalar(
-                    out=dst,
-                    in0=src,
-                    scalar1=mvs[g][:, i, 0:1],
-                    scalar2=rstds[g][:, i : i + 1],
-                    op0=ALU.subtract,
-                    op1=ALU.mult,
-                )
-            else:
+            if on_scalar(g, i):
                 nc.scalar.activation(
                     out=dst,
                     in_=src,
                     func=ACT.Identity,
                     scale=rstds[g][:, i : i + 1],
                     bias=nmrs[g][:, i : i + 1],
+                )
+            else:
+                nc.gpsimd.tensor_scalar(
+                    out=dst,
+                    in0=src,
+                    scalar1=mvs[g][:, i, 0:1],
+                    scalar2=rstds[g][:, i : i + 1],
+                    op0=ALU.subtract,
+                    op1=ALU.mult,
                 )
 
         def transposes(u, j):
@@ -150,49 +146,33 @@ def tile_toyattnsublayer_pa_t_kernel(tc, h, ln_w, ln_b, w_q, w_k, w_v, out_0, ou
             for i in range(GT):
                 nc.tensor.transpose(tp[:, P * i : P * (i + 1)], xhs[g][:, i, j, P * c : P * (c + 1)], ident_f[:])
 
-        def leave(u, j, on_vector):
+        def leave(u, j):
             kb = 4 * (u % NC) + j
             if u not in pls:
                 pls[u] = plpool.tile([P, 4, GTOK], BF16, name="pl")
-            if on_vector:
-                nc.vector.tensor_scalar(
-                    out=pls[u][:, j, :],
-                    in0=tps[(u, j)][:],
-                    scalar1=wb[:, kb : kb + 1],
-                    scalar2=wb[:, 8 + kb : 9 + kb],
-                    op0=ALU.mult,
-                    op1=ALU.add,
-                )
-            else:
-                nc.scalar.activation(
-                    out=pls[u][:, j, :],
-                    in_=tps[(u, j)][:],
-                    func=ACT.Identity,
-                    scale=wb[:, kb : kb + 1],
-                    bias=wb[:, 8 + kb : 9 + kb],
-                )
-
-        def pieces(u):
-            n = 2 if u == NU - 1 else 1
-            return [slice(GTOK // n * a, GTOK // n * (a + 1)) for a in range(n)]
+            nc.scalar.activation(
+                out=pls[u][:, j, :],
+                in_=tps[(u, j)][:],
+                func=ACT.Identity,
+                scale=wb[:, kb : kb + 1],
+                bias=wb[:, 8 + kb : 9 + kb],
+            )
 
         def regroup(u):
             grs[u] = grpool.tile([P, GTOK, 4], BF16, name="gr", align_bytes=64)
-            for tok in pieces(u):
-                nc.vector.tensor_copy(
-                    out=grs[u][:, tok, :].rearrange("p (c i) t -> p c t i", i=4),
-                    in_=pls[u][:, :, tok].rearrange("p t (c i) -> p c t i", i=4),
-                )
+            nc.vector.tensor_copy(
+                out=grs[u][:].rearrange("p (c i) t -> p c t i", i=4),
+                in_=pls[u][:].rearrange("p t (c i) -> p c t i", i=4),
+            )
 
         def quantise(u):
             cds[u] = cpool.tile([P, GTOK], U32, name="codes", align_bytes=64)
             scs[u] = cpool.tile([P, GTOK], U8, name="scl", align_bytes=64)
-            for tok in pieces(u):
-                nc.vector.quantize_mx(
-                    out=cds[u][:, tok].bitcast(FP8X4),
-                    scales=scs[u][:, tok],
-                    in_=grs[u][:, tok, :].rearrange("p n j -> p (n j)"),
-                )
+            nc.vector.quantize_mx(
+                out=cds[u][:].bitcast(FP8X4),
+                scales=scs[u][:],
+                in_=grs[u][:].rearrange("p n j -> p (n j)"),
+            )
 
         def multiply(u):
             g, c = divmod(u, NC)
@@ -209,10 +189,11 @@ def tile_toyattnsublayer_pa_t_kernel(tc, h, ln_w, ln_b, w_q, w_k, w_v, out_0, ou
                     stop=(c == NC - 1),
                 )
 
-        def out_copy(g, i, on_vector):
+        def out_copy(g, i):
             if g not in osts:
                 osts[g] = opool.tile([P, 3, GT, E], F32, name="ost")
             src = accs[g][i][:, 0 : 3 * E].rearrange("p (s e) -> p s e", s=3)
+            on_vector = i % 2 == 0 if g == NG - 1 else vector_out(g)
             if on_vector:
                 nc.vector.tensor_copy(out=osts[g][:, :, i, :], in_=src)
             else:
@@ -228,112 +209,98 @@ def tile_toyattnsublayer_pa_t_kernel(tc, h, ln_w, ln_b, w_q, w_k, w_v, out_0, ou
         make_identity(nc, ident_f[:])
         lnrows = const.tile([P, P], BF16, name="lnrows")
         nc.vector.memset(lnrows[:], 0.0)
+        eps_t = const.tile([P, 1], F32, name="eps_t")
+        nc.vector.memset(eps_t[:], 0.0)
+        nc.vector.tensor_scalar(out=eps_t[:], in0=eps_t[:], scalar1=EPS, scalar2=None, op0=ALU.add)
         wg = const.tile([P, NC, 512, 4], BF16, name="wg", align_bytes=64)
         nc.vector.memset(wg[:, :, 3 * E : 512, :], 0.0)
 
-        load(0, (0, 1))
+        load(0, range(GT))
         for r, vec in enumerate((ln_w, ln_b)):
             for c in range(NC):
                 nc.sync.dma_start(
                     out=lnrows[8 * r + 4 * c : 8 * r + 4 * (c + 1), :].rearrange("j (b r) -> j b r", r=8),
                     in_=vec[KP * c : KP * (c + 1)].rearrange("(b j r) -> j b r", j=4, r=8),
                 )
-        load(0, (2, 3))
-        load(1)
         wraw = const.tile([P, 3, D], BF16, name="wraw")
         for s, w in enumerate((w_q, w_k, w_v)):
             nc.sync.dma_start(out=wraw[:, s, :], in_=w)
+        load(1, range(GT))
         for g in range(2, HBUFS):
             load(g)
-        wslots = const.tile([P, 3, 4, D // 4], BF16, name="wslots")
 
-        ln_ps = psum.tile([P, P], BF16, name="ln_ps", tag="O2")
-        nc.tensor.transpose(ln_ps[:], lnrows[:], ident_b[:])
-        wb = const.tile([P, 16], F32, name="wb")
-        nc.scalar.copy(out=wb[:], in_=ln_ps[:, 0:16])
+        wslots = const.tile([P, 3, 4, D // 4], BF16, name="wslots")
         for s in range(3):
-            nc.scalar.copy(
+            nc.gpsimd.tensor_scalar(
                 out=wslots[:, s, :, :].rearrange("p j (b r) -> p j b r", r=8),
-                in_=wraw[:, s, :].rearrange("p (b j r) -> p j b r", j=4, r=8),
+                in0=wraw[:, s, :].rearrange("p (b j r) -> p j b r", j=4, r=8),
+                scalar1=1.0,
+                scalar2=0.0,
+                op0=ALU.mult,
+                op1=ALU.add,
             )
+        wb = const.tile([P, 16], F32, name="wb")
         wtags = ("T0", "T1", "T2", "T3", "O0", "O1")
-        for c in range(NC):
-            for s in range(3):
-                wt = psum.tile([P, 4, E], BF16, name="wt", tag=wtags[3 * c + s])
-                for j in range(4):
-                    nc.tensor.transpose(wt[:, j, :], wslots[:, s, j, P * c : P * (c + 1)], ident_b[:])
-                nc.scalar.copy(out=wg[:, c, E * s : E * (s + 1), :], in_=wt[:].rearrange("p j e -> p e j"))
         wcodes = const.tile([P, NC, 512], U32, name="wcodes", align_bytes=64)
         wscales = const.tile([P, NC, 512], U8, name="wscales", align_bytes=64)
 
-        for t in range(-A0, NU + ML + 1):
-            in_u = 0 <= t < NU
-            prev_u = 0 <= t - 1 < NU
-            g_bs = group_of(t, BS)
-            g_bv = group_of(t, BV)
-            g_f = group_of(t, -(ML + 2))
-            g_ve = group_of(t, VE)
-            g_sq = group_of(t, SQ)
-            g_rc = group_of(t, RC)
-            g_s, second = divmod(t + A0, 2)
-            have_s = 0 <= g_s < NG
-            pairs = [(2 * second + i, a) for i in range(2) for a in range(2)]
-            n_fs = GT - n_vector_out(g_f) if g_f is not None else 0
+        def weights_to_slots():
+            ln_ps = psum.tile([P, P], BF16, name="ln_ps", tag="O2")
+            nc.tensor.transpose(ln_ps[:], lnrows[:], ident_b[:])
+            nc.scalar.copy(out=wb[:], in_=ln_ps[:, 0:16])
+            for c in range(NC):
+                for s in range(3):
+                    wt = psum.tile([P, 4, E], BF16, name="wt", tag=wtags[3 * c + s])
+                    for j in range(4):
+                        nc.tensor.transpose(wt[:, j, :], wslots[:, s, j, P * c : P * (c + 1)], ident_b[:])
+                    nc.scalar.copy(out=wg[:, c, E * s : E * (s + 1), :], in_=wt[:].rearrange("p j e -> p e j"))
 
-            if g_sq is not None:
-                root(g_sq)
-            if g_bs is not None:
-                for i in range(n_scalar_norm(g_bs)):
-                    normalise(g_bs, GT - 1 - i, False)
-                if g_bs + HBUFS < NG:
-                    load(g_bs + HBUFS)
-            if prev_u:
-                regroup(t - 1)
-            for j in range(2):
+        for t in range(-ST, NU + ML + 1):
+            in_u = 0 <= t < NU
+            next_u = 0 <= t + 1 < NU
+            s_half = half_of(t, ST)
+            n_half = half_of(t, NM)
+            g_out, odd = divmod(t - ML - 2, 2)
+            do_out = odd == 0 and 0 <= g_out < NG
+
+            for j in range(4):
                 if in_u:
-                    leave(t, j, False)
-                if -1 <= t < NU - 1:
+                    leave(t, j)
+                if j == 1:
+                    if n_half is not None:
+                        root(*n_half)
+                    if do_out:
+                        for i in range(GT):
+                            out_copy(g_out, i)
+                        store(g_out)
+                    if 0 <= t - ML < NU:
+                        quantise(t - ML)
+                        multiply(t - ML)
+                if next_u:
                     transposes(t + 1, j)
-            if g_f is not None:
-                for i in range(GT):
-                    out_copy(g_f, i, i >= n_fs)
-                store(g_f)
-            if 0 <= t - ML < NU:
-                multiply(t - ML)
-            if g_ve is not None:
-                add_eps(g_ve)
-            if g_rc is not None:
-                reciprocal(g_rc)
-            if have_s:
-                stats(g_s, pairs[0:2])
-            if t == -2:
+            if 0 <= t - 1 < NU:
+                regroup(t - 1)
+            if n_half is not None:
+                g, tiles = n_half
+                reciprocal(g, tiles)
+                for i in tiles:
+                    if on_scalar(g, i):
+                        neg_mean_rstd(g, i)
+                for i in tiles:
+                    normalise(g, i)
+                if tiles[-1] == GT - 1 and g + HBUFS < NG:
+                    load(g + HBUFS)
+            if s_half is not None:
+                g, tiles = s_half
+                for i in tiles:
+                    stats(g, i)
+                for i in tiles:
+                    aggregate(g, i)
+            if t == -NM + 1:
+                weights_to_slots()
+            if t == 0:
                 nc.vector.quantize_mx(
                     out=wcodes[:].rearrange("p c n -> p (c n)").bitcast(FP8X4),
                     scales=wscales[:].rearrange("p c n -> p (c n)"),
                     in_=wg[:].rearrange("p c n j -> p (c n j)"),
                 )
-            n_vl = n_vector_leave(t) if in_u else 0
-            if not have_s:
-                if g_bv is not None:
-                    for i in range(GT - n_scalar_norm(g_bv)):
-                        normalise(g_bv, i, True)
-                for j in range(4 - n_vl, 4):
-                    leave(t, j, True)
-                    if t < NU - 1:
-                        transposes(t + 1, j)
-            if prev_u:
-                quantise(t - 1)
-            if g_rc is not None:
-                neg_mean_rstd(g_rc)
-            for j in range(2, 4 - n_vl):
-                if in_u:
-                    leave(t, j, False)
-                if -1 <= t < NU - 1:
-                    transposes(t + 1, j)
-            if have_s:
-                stats(g_s, pairs[2:4])
-                if g_bv is not None:
-                    for i in range(GT - n_scalar_norm(g_bv)):
-                        normalise(g_bv, i, True)
-            if have_s and second == 1:
-                aggregate(g_s)

@@ -64,7 +64,7 @@ def tile_toyattnsublayer_pa_t_kernel(tc, h, ln_w, ln_b, w_q, w_k, w_v, out_0, ou
         psum = ctx.enter_context(tc.psum_pool(name="psum", bufs=1))
         ctx.enter_context(tc.manual_schedule())
 
-        hts, sts, mvs, stds, rstds, nmrs, xhs = {}, {}, {}, {}, {}, {}, {}
+        hts, sts, mvs, stds, rstds, nmrs, nmus, xhs = {}, {}, {}, {}, {}, {}, {}, {}
         tps, pls, grs, cds, scs, accs, osts = {}, {}, {}, {}, {}, {}, {}
 
         def load(g, tiles=None):
@@ -116,6 +116,14 @@ def tile_toyattnsublayer_pa_t_kernel(tc, h, ln_w, ln_b, w_q, w_k, w_v, out_0, ou
                 op1=ALU.mult,
             )
 
+        def neg_mean(g, tiles):
+            if g not in nmus:
+                nmus[g] = small.tile([P, GT], F32, name="nmu")
+            cols = slice(tiles[0], tiles[-1] + 1)
+            nc.gpsimd.tensor_scalar(
+                out=nmus[g][:, cols], in0=mvs[g][:, cols, 0], scalar1=-1.0, scalar2=0.0, op0=ALU.mult, op1=ALU.add
+            )
+
         def normalise(g, i):
             if g not in xhs:
                 xhs[g] = xpool.tile([P, GT, 4, D // 4], F32, name="xh")
@@ -133,9 +141,9 @@ def tile_toyattnsublayer_pa_t_kernel(tc, h, ln_w, ln_b, w_q, w_k, w_v, out_0, ou
                 nc.gpsimd.tensor_scalar(
                     out=dst,
                     in0=src,
-                    scalar1=mvs[g][:, i, 0:1],
+                    scalar1=nmus[g][:, i : i + 1],
                     scalar2=rstds[g][:, i : i + 1],
-                    op0=ALU.subtract,
+                    op0=ALU.add,
                     op1=ALU.mult,
                 )
 
@@ -282,6 +290,8 @@ def tile_toyattnsublayer_pa_t_kernel(tc, h, ln_w, ln_b, w_q, w_k, w_v, out_0, ou
                 regroup(t - 1)
             if n_half is not None:
                 g, tiles = n_half
+                if not all(on_scalar(g, i) for i in tiles):
+                    neg_mean(g, tiles)
                 reciprocal(g, tiles)
                 for i in tiles:
                     if on_scalar(g, i):

@@ -25,8 +25,11 @@ NC = D // KP
 NU = NG * NC
 HBUFS = 8
 
-ST = 4
+ST = 5
+RT = 4
 NM = 3
+NS = 2
+SHARED = 1
 ML = 2
 
 
@@ -34,8 +37,8 @@ def on_scalar(g, i):
     if g == 0:
         return True
     if g == 1:
-        return i < 2
-    return i == 0
+        return i >= 2
+    return i == GT - 1
 
 
 def vector_out(g):
@@ -124,11 +127,11 @@ def tile_toyattnsublayer_pa_t_kernel(tc, h, ln_w, ln_b, w_q, w_k, w_v, out_0, ou
                 out=nmus[g][:, cols], in0=mvs[g][:, cols, 0], scalar1=-1.0, scalar2=0.0, op0=ALU.mult, op1=ALU.add
             )
 
-        def normalise(g, i):
+        def normalise(g, i, js=slice(0, 4)):
             if g not in xhs:
                 xhs[g] = xpool.tile([P, GT, 4, D // 4], F32, name="xh")
-            src = hts[g][:, i, :].rearrange("p (b j r) -> p j b r", j=4, r=8)
-            dst = xhs[g][:, i, :, :].rearrange("p j (b r) -> p j b r", r=8)
+            src = hts[g][:, i, :].rearrange("p (b j r) -> p j b r", j=4, r=8)[:, js, :, :]
+            dst = xhs[g][:, i, js, :].rearrange("p j (b r) -> p j b r", r=8)
             if on_scalar(g, i):
                 nc.scalar.activation(
                     out=dst,
@@ -267,16 +270,23 @@ def tile_toyattnsublayer_pa_t_kernel(tc, h, ln_w, ln_b, w_q, w_k, w_v, out_0, ou
             in_u = 0 <= t < NU
             next_u = 0 <= t + 1 < NU
             s_half = half_of(t, ST)
+            r_half = half_of(t, RT)
             n_half = half_of(t, NM)
+            ns_half = half_of(t, NS)
             g_out, odd = divmod(t - ML - 2, 2)
             do_out = odd == 0 and 0 <= g_out < NG
 
+            if ns_half is not None:
+                g, tiles = ns_half
+                for i in tiles:
+                    if on_scalar(g, i):
+                        normalise(g, i)
             for j in range(4):
                 if in_u:
                     leave(t, j)
                 if j == 1:
-                    if n_half is not None:
-                        root(*n_half)
+                    if r_half is not None:
+                        root(*r_half)
                     if do_out:
                         for i in range(GT):
                             out_copy(g_out, i)
@@ -286,27 +296,36 @@ def tile_toyattnsublayer_pa_t_kernel(tc, h, ln_w, ln_b, w_q, w_k, w_v, out_0, ou
                         multiply(t - ML)
                 if next_u:
                     transposes(t + 1, j)
-            if 0 <= t - 1 < NU:
-                regroup(t - 1)
             if n_half is not None:
                 g, tiles = n_half
                 if not all(on_scalar(g, i) for i in tiles):
                     neg_mean(g, tiles)
                 reciprocal(g, tiles)
+            if 0 <= t - 1 < NU:
+                regroup(t - 1)
+            if n_half is not None:
+                g, tiles = n_half
+                if tiles[0] == 0 and not on_scalar(g, 0):
+                    normalise(g, 0)
+                    normalise(g, SHARED, slice(0, 2))
+                elif tiles[0] != 0 and not on_scalar(g, SHARED):
+                    normalise(g, SHARED, slice(2, 4))
+                for i in tiles:
+                    if i > SHARED and not on_scalar(g, i):
+                        normalise(g, i)
                 for i in tiles:
                     if on_scalar(g, i):
                         neg_mean_rstd(g, i)
-                for i in tiles:
-                    normalise(g, i)
-                if tiles[-1] == GT - 1 and g + HBUFS < NG:
-                    load(g + HBUFS)
             if s_half is not None:
                 g, tiles = s_half
                 for i in tiles:
                     stats(g, i)
                 for i in tiles:
                     aggregate(g, i)
-            if t == -NM + 1:
+            g_done, odd = divmod(t + 1, 2)
+            if odd == 0 and 0 <= g_done < NG - HBUFS:
+                load(g_done + HBUFS)
+            if t == -NS:
                 weights_to_slots()
             if t == 0:
                 nc.vector.quantize_mx(

@@ -30,6 +30,9 @@ RT = 4
 NM = 3
 NS = 2
 SHARED = 1
+VTOK = 384
+U_ALL = 22
+G_OUT = 12
 ML = 2
 
 
@@ -39,10 +42,6 @@ def on_scalar(g, i):
     if g == 1:
         return i >= 2
     return i == GT - 1
-
-
-def vector_out(g):
-    return 2 * g + ML + 2 >= 2 * NG - ST + 2
 
 
 def half_of(t, lead):
@@ -67,7 +66,7 @@ def tile_toyattnsublayer_pa_t_kernel(tc, h, ln_w, ln_b, w_q, w_k, w_v, out_0, ou
         psum = ctx.enter_context(tc.psum_pool(name="psum", bufs=1))
         ctx.enter_context(tc.manual_schedule())
 
-        hts, sts, mvs, stds, rstds, nmrs, nmus, xhs = {}, {}, {}, {}, {}, {}, {}, {}
+        hts, sts, mvs, stds, rstds, nmrs, xhs = {}, {}, {}, {}, {}, {}, {}
         tps, pls, grs, cds, scs, accs, osts = {}, {}, {}, {}, {}, {}, {}
 
         def load(g, tiles=None):
@@ -106,25 +105,17 @@ def tile_toyattnsublayer_pa_t_kernel(tc, h, ln_w, ln_b, w_q, w_k, w_v, out_0, ou
             cols = slice(tiles[0], tiles[-1] + 1)
             nc.vector.reciprocal(rstds[g][:, cols], stds[g][:, cols])
 
-        def neg_mean_rstd(g, i):
+        def neg_mean_rstd(g, tiles):
             if g not in nmrs:
                 nmrs[g] = small.tile([P, GT], F32, name="nmr")
-            eng = nc.vector if g == 0 else nc.gpsimd
-            eng.tensor_scalar(
-                out=nmrs[g][:, i : i + 1],
-                in0=mvs[g][:, i, 0:1],
-                scalar1=rstds[g][:, i : i + 1],
-                scalar2=-1.0,
+            cols = slice(tiles[0], tiles[-1] + 1)
+            nc.vector.scalar_tensor_tensor(
+                out=nmrs[g][:, cols],
+                in0=mvs[g][:, cols, 0],
+                scalar=-1.0,
+                in1=rstds[g][:, cols],
                 op0=ALU.mult,
                 op1=ALU.mult,
-            )
-
-        def neg_mean(g, tiles):
-            if g not in nmus:
-                nmus[g] = small.tile([P, GT], F32, name="nmu")
-            cols = slice(tiles[0], tiles[-1] + 1)
-            nc.gpsimd.tensor_scalar(
-                out=nmus[g][:, cols], in0=mvs[g][:, cols, 0], scalar1=-1.0, scalar2=0.0, op0=ALU.mult, op1=ALU.add
             )
 
         def normalise(g, i, js=slice(0, 4)):
@@ -144,10 +135,10 @@ def tile_toyattnsublayer_pa_t_kernel(tc, h, ln_w, ln_b, w_q, w_k, w_v, out_0, ou
                 nc.gpsimd.tensor_scalar(
                     out=dst,
                     in0=src,
-                    scalar1=nmus[g][:, i : i + 1],
-                    scalar2=rstds[g][:, i : i + 1],
-                    op0=ALU.add,
-                    op1=ALU.mult,
+                    scalar1=rstds[g][:, i : i + 1],
+                    scalar2=nmrs[g][:, i : i + 1],
+                    op0=ALU.mult,
+                    op1=ALU.add,
                 )
 
         def transposes(u, j):
@@ -169,27 +160,30 @@ def tile_toyattnsublayer_pa_t_kernel(tc, h, ln_w, ln_b, w_q, w_k, w_v, out_0, ou
                 bias=wb[:, 8 + kb : 9 + kb],
             )
 
-        def regroup(u):
-            grs[u] = grpool.tile([P, GTOK, 4], BF16, name="gr", align_bytes=64)
-            nc.vector.tensor_copy(
-                out=grs[u][:].rearrange("p (c i) t -> p c t i", i=4),
-                in_=pls[u][:].rearrange("p t (c i) -> p c t i", i=4),
+        def regroup(u, on_vector, tok):
+            if u not in grs:
+                grs[u] = grpool.tile([P, GTOK, 4], BF16, name="gr", align_bytes=64)
+            copy = nc.vector.tensor_copy if on_vector else nc.scalar.copy
+            copy(
+                out=grs[u][:, tok, :].rearrange("p (c i) t -> p c t i", i=4),
+                in_=pls[u][:, :, tok].rearrange("p t (c i) -> p c t i", i=4),
             )
 
-        def quantise(u):
-            cds[u] = cpool.tile([P, GTOK], U32, name="codes", align_bytes=64)
-            scs[u] = cpool.tile([P, GTOK], U8, name="scl", align_bytes=64)
+        def quantise(u, tok):
+            if u not in cds:
+                cds[u] = cpool.tile([P, GTOK], U32, name="codes", align_bytes=64)
+                scs[u] = cpool.tile([P, GTOK], U8, name="scl", align_bytes=64)
             nc.vector.quantize_mx(
-                out=cds[u][:].bitcast(FP8X4),
-                scales=scs[u][:],
-                in_=grs[u][:].rearrange("p n j -> p (n j)"),
+                out=cds[u][:, tok].bitcast(FP8X4),
+                scales=scs[u][:, tok],
+                in_=grs[u][:, tok, :].rearrange("p n j -> p (n j)"),
             )
 
-        def multiply(u):
+        def multiply(u, tiles):
             g, c = divmod(u, NC)
             if c == 0:
                 accs[g] = [psum.tile([P, 512], F32, name="acc%d" % i, tag="O%d" % i) for i in range(GT)]
-            for i in range(GT):
+            for i in tiles:
                 nc.tensor.matmul_mx(
                     out=accs[g][i][:],
                     lhsT=cds[u][:, P * i : P * (i + 1)].bitcast(FP8X4),
@@ -204,8 +198,7 @@ def tile_toyattnsublayer_pa_t_kernel(tc, h, ln_w, ln_b, w_q, w_k, w_v, out_0, ou
             if g not in osts:
                 osts[g] = opool.tile([P, 3, GT, E], F32, name="ost")
             src = accs[g][i][:, 0 : 3 * E].rearrange("p (s e) -> p s e", s=3)
-            on_vector = i % 2 == 0 if g == NG - 1 else vector_out(g)
-            if on_vector:
+            if i % 2 == 0 if g == NG - 1 else g >= G_OUT:
                 nc.vector.tensor_copy(out=osts[g][:, :, i, :], in_=src)
             else:
                 nc.scalar.copy(out=osts[g][:, :, i, :], in_=src)
@@ -284,25 +277,43 @@ def tile_toyattnsublayer_pa_t_kernel(tc, h, ln_w, ln_b, w_q, w_k, w_v, out_0, ou
             for j in range(4):
                 if in_u:
                     leave(t, j)
-                if j == 1:
-                    if r_half is not None:
-                        root(*r_half)
-                    if do_out:
-                        for i in range(GT):
-                            out_copy(g_out, i)
-                        store(g_out)
-                    if 0 <= t - ML < NU:
-                        quantise(t - ML)
-                        multiply(t - ML)
+                if j == 0 and 0 <= t - 1 < U_ALL:
+                    regroup(t - 1, False, slice(VTOK, GTOK))
+                if j == 1 and do_out and g_out < G_OUT:
+                    for i in range(GT):
+                        out_copy(g_out, i)
+                    store(g_out)
                 if next_u:
                     transposes(t + 1, j)
+            if 0 <= t - ML < NU - 1:
+                quantise(t - ML, slice(0, GTOK))
+                if not (do_out and g_out >= G_OUT):
+                    multiply(t - ML, range(GT))
             if n_half is not None:
-                g, tiles = n_half
-                if not all(on_scalar(g, i) for i in tiles):
-                    neg_mean(g, tiles)
-                reciprocal(g, tiles)
-            if 0 <= t - 1 < NU:
-                regroup(t - 1)
+                reciprocal(*n_half)
+            if r_half is not None:
+                g, tiles = r_half
+                for i in tiles:
+                    aggregate(g, i)
+                root(g, tiles)
+            if n_half is not None:
+                neg_mean_rstd(*n_half)
+            if 0 <= t - 1 < NU - 1:
+                regroup(t - 1, True, slice(0, VTOK if t - 1 < U_ALL else GTOK))
+            if t - 1 == NU - 1:
+                halves = [slice(GTOK // 2 * a, GTOK // 2 * (a + 1)) for a in range(2)]
+                for tok in halves:
+                    regroup(t - 1, True, tok)
+                for a in range(2):
+                    quantise(t - 1, halves[a])
+            if do_out and g_out >= G_OUT:
+                for i in range(GT):
+                    out_copy(g_out, i)
+                store(g_out)
+                if t - ML < NU:
+                    multiply(t - ML, range(GT))
+            if t - 1 == NU - 1:
+                multiply(t - 1, range(GT))
             if n_half is not None:
                 g, tiles = n_half
                 if tiles[0] == 0 and not on_scalar(g, 0):
@@ -313,15 +324,10 @@ def tile_toyattnsublayer_pa_t_kernel(tc, h, ln_w, ln_b, w_q, w_k, w_v, out_0, ou
                 for i in tiles:
                     if i > SHARED and not on_scalar(g, i):
                         normalise(g, i)
-                for i in tiles:
-                    if on_scalar(g, i):
-                        neg_mean_rstd(g, i)
             if s_half is not None:
                 g, tiles = s_half
                 for i in tiles:
                     stats(g, i)
-                for i in tiles:
-                    aggregate(g, i)
             g_done, odd = divmod(t + 1, 2)
             if odd == 0 and 0 <= g_done < NG - HBUFS:
                 load(g_done + HBUFS)

@@ -29,19 +29,12 @@ ST = 5
 RT = 4
 NM = 3
 NS = 2
-SHARED = 1
-VTOK = 384
-U_ALL = 22
 G_OUT = 12
 ML = 2
 
 
 def on_scalar(g, i):
-    if g == 0:
-        return True
-    if g == 1:
-        return i >= 2
-    return i == GT - 1
+    return g == 0 or i % 2 == 1
 
 
 def half_of(t, lead):
@@ -118,11 +111,11 @@ def tile_toyattnsublayer_pa_t_kernel(tc, h, ln_w, ln_b, w_q, w_k, w_v, out_0, ou
                 op1=ALU.mult,
             )
 
-        def normalise(g, i, js=slice(0, 4)):
+        def normalise(g, i):
             if g not in xhs:
                 xhs[g] = xpool.tile([P, GT, 4, D // 4], F32, name="xh")
-            src = hts[g][:, i, :].rearrange("p (b j r) -> p j b r", j=4, r=8)[:, js, :, :]
-            dst = xhs[g][:, i, js, :].rearrange("p j (b r) -> p j b r", r=8)
+            src = hts[g][:, i, :].rearrange("p (b j r) -> p j b r", j=4, r=8)
+            dst = xhs[g][:, i, :, :].rearrange("p j (b r) -> p j b r", r=8)
             if on_scalar(g, i):
                 nc.scalar.activation(
                     out=dst,
@@ -160,11 +153,10 @@ def tile_toyattnsublayer_pa_t_kernel(tc, h, ln_w, ln_b, w_q, w_k, w_v, out_0, ou
                 bias=wb[:, 8 + kb : 9 + kb],
             )
 
-        def regroup(u, on_vector, tok):
+        def regroup(u, tok):
             if u not in grs:
                 grs[u] = grpool.tile([P, GTOK, 4], BF16, name="gr", align_bytes=64)
-            copy = nc.vector.tensor_copy if on_vector else nc.scalar.copy
-            copy(
+            nc.vector.tensor_copy(
                 out=grs[u][:, tok, :].rearrange("p (c i) t -> p c t i", i=4),
                 in_=pls[u][:, :, tok].rearrange("p t (c i) -> p c t i", i=4),
             )
@@ -181,11 +173,11 @@ def tile_toyattnsublayer_pa_t_kernel(tc, h, ln_w, ln_b, w_q, w_k, w_v, out_0, ou
 
         def multiply(u, tiles):
             g, c = divmod(u, NC)
-            if c == 0:
-                accs[g] = [psum.tile([P, 512], F32, name="acc%d" % i, tag="O%d" % i) for i in range(GT)]
             for i in tiles:
+                if c == 0:
+                    accs[(g, i)] = psum.tile([P, 512], F32, name="acc", tag="O%d" % i)
                 nc.tensor.matmul_mx(
-                    out=accs[g][i][:],
+                    out=accs[(g, i)][:],
                     lhsT=cds[u][:, P * i : P * (i + 1)].bitcast(FP8X4),
                     lhsT_scale=scs[u][:, P * i : P * (i + 1)],
                     rhs=wcodes[:, c, :].bitcast(FP8X4),
@@ -197,7 +189,7 @@ def tile_toyattnsublayer_pa_t_kernel(tc, h, ln_w, ln_b, w_q, w_k, w_v, out_0, ou
         def out_copy(g, i):
             if g not in osts:
                 osts[g] = opool.tile([P, 3, GT, E], F32, name="ost")
-            src = accs[g][i][:, 0 : 3 * E].rearrange("p (s e) -> p s e", s=3)
+            src = accs[(g, i)][:, 0 : 3 * E].rearrange("p (s e) -> p s e", s=3)
             if i % 2 == 0 if g == NG - 1 else g >= G_OUT:
                 nc.vector.tensor_copy(out=osts[g][:, :, i, :], in_=src)
             else:
@@ -266,8 +258,8 @@ def tile_toyattnsublayer_pa_t_kernel(tc, h, ln_w, ln_b, w_q, w_k, w_v, out_0, ou
             r_half = half_of(t, RT)
             n_half = half_of(t, NM)
             ns_half = half_of(t, NS)
-            g_out, odd = divmod(t - ML - 2, 2)
-            do_out = odd == 0 and 0 <= g_out < NG
+            g_out, odd_out = divmod(t - ML - 2, 2)
+            do_out = odd_out == 0 and 0 <= g_out < NG
 
             if ns_half is not None:
                 g, tiles = ns_half
@@ -277,18 +269,21 @@ def tile_toyattnsublayer_pa_t_kernel(tc, h, ln_w, ln_b, w_q, w_k, w_v, out_0, ou
             for j in range(4):
                 if in_u:
                     leave(t, j)
-                if j == 0 and 0 <= t - 1 < U_ALL:
-                    regroup(t - 1, False, slice(VTOK, GTOK))
-                if j == 1 and do_out and g_out < G_OUT:
-                    for i in range(GT):
+                if j == 1 and 0 <= g_out < G_OUT:
+                    for i in (2 * odd_out, 2 * odd_out + 1):
                         out_copy(g_out, i)
-                    store(g_out)
+                    if odd_out:
+                        store(g_out)
                 if next_u:
                     transposes(t + 1, j)
             if 0 <= t - ML < NU - 1:
                 quantise(t - ML, slice(0, GTOK))
-                if not (do_out and g_out >= G_OUT):
+                if odd_out:
+                    if g_out < G_OUT:
+                        multiply(t - ML - 1, (2, 3))
                     multiply(t - ML, range(GT))
+                elif g_out < G_OUT:
+                    multiply(t - ML, (0, 1))
             if n_half is not None:
                 reciprocal(*n_half)
             if r_half is not None:
@@ -299,11 +294,11 @@ def tile_toyattnsublayer_pa_t_kernel(tc, h, ln_w, ln_b, w_q, w_k, w_v, out_0, ou
             if n_half is not None:
                 neg_mean_rstd(*n_half)
             if 0 <= t - 1 < NU - 1:
-                regroup(t - 1, True, slice(0, VTOK if t - 1 < U_ALL else GTOK))
+                regroup(t - 1, slice(0, GTOK))
             if t - 1 == NU - 1:
                 halves = [slice(GTOK // 2 * a, GTOK // 2 * (a + 1)) for a in range(2)]
                 for tok in halves:
-                    regroup(t - 1, True, tok)
+                    regroup(t - 1, tok)
                 for a in range(2):
                     quantise(t - 1, halves[a])
             if do_out and g_out >= G_OUT:
@@ -316,13 +311,8 @@ def tile_toyattnsublayer_pa_t_kernel(tc, h, ln_w, ln_b, w_q, w_k, w_v, out_0, ou
                 multiply(t - 1, range(GT))
             if n_half is not None:
                 g, tiles = n_half
-                if tiles[0] == 0 and not on_scalar(g, 0):
-                    normalise(g, 0)
-                    normalise(g, SHARED, slice(0, 2))
-                elif tiles[0] != 0 and not on_scalar(g, SHARED):
-                    normalise(g, SHARED, slice(2, 4))
                 for i in tiles:
-                    if i > SHARED and not on_scalar(g, i):
+                    if not on_scalar(g, i):
                         normalise(g, i)
             if s_half is not None:
                 g, tiles = s_half

@@ -34,7 +34,7 @@ ML = 2
 
 
 def on_scalar(g, i):
-    return g == 0 or i % 2 == 1
+    return i % 2 == 1
 
 
 def half_of(t, lead):
@@ -138,6 +138,7 @@ def tile_toyattnsublayer_pa_t_kernel(tc, h, ln_w, ln_b, w_q, w_k, w_v, out_0, ou
             g, c = divmod(u, NC)
             tp = psum.tile([P, GTOK], F32, name="tp", tag="T%d" % j)
             tps[(u, j)] = tp
+            nc.tensor.matmul(tp[:, 0:P], lhsT=ident_f[:], rhs=ident_f[:], start=True, stop=True)
             for i in range(GT):
                 nc.tensor.transpose(tp[:, P * i : P * (i + 1)], xhs[g][:, i, j, P * c : P * (c + 1)], ident_f[:])
 
@@ -190,7 +191,7 @@ def tile_toyattnsublayer_pa_t_kernel(tc, h, ln_w, ln_b, w_q, w_k, w_v, out_0, ou
             if g not in osts:
                 osts[g] = opool.tile([P, 3, GT, E], F32, name="ost")
             src = accs[(g, i)][:, 0 : 3 * E].rearrange("p (s e) -> p s e", s=3)
-            if i % 2 == 0 if g == NG - 1 else g >= G_OUT:
+            if i % 2 == 0 if g == NG - 1 else G_OUT <= g < NG - 2:
                 nc.vector.tensor_copy(out=osts[g][:, :, i, :], in_=src)
             else:
                 nc.scalar.copy(out=osts[g][:, :, i, :], in_=src)
@@ -236,28 +237,30 @@ def tile_toyattnsublayer_pa_t_kernel(tc, h, ln_w, ln_b, w_q, w_k, w_v, out_0, ou
                 op1=ALU.add,
             )
         wb = const.tile([P, 16], F32, name="wb")
-        wtags = ("T0", "T1", "T2", "T3", "O0", "O1")
         wcodes = const.tile([P, NC, 512], U32, name="wcodes", align_bytes=64)
         wscales = const.tile([P, NC, 512], U8, name="wscales", align_bytes=64)
 
-        def weights_to_slots():
+        def gain_and_bias():
             ln_ps = psum.tile([P, P], BF16, name="ln_ps", tag="O2")
             nc.tensor.transpose(ln_ps[:], lnrows[:], ident_b[:])
             nc.scalar.copy(out=wb[:], in_=ln_ps[:, 0:16])
+
+        def turn_weights(s):
             for c in range(NC):
-                for s in range(3):
-                    wt = psum.tile([P, 4, E], BF16, name="wt", tag=wtags[3 * c + s])
-                    for j in range(4):
-                        nc.tensor.transpose(wt[:, j, :], wslots[:, s, j, P * c : P * (c + 1)], ident_b[:])
-                    nc.scalar.copy(out=wg[:, c, E * s : E * (s + 1), :], in_=wt[:].rearrange("p j e -> p e j"))
+                wt = psum.tile([P, 4, E], BF16, name="wt", tag="O%d" % ((NC * s + c) % GT))
+                for j in range(4):
+                    nc.tensor.transpose(wt[:, j, :], wslots[:, s, j, P * c : P * (c + 1)], ident_b[:])
+                nc.scalar.copy(out=wg[:, c, E * s : E * (s + 1), :], in_=wt[:].rearrange("p j e -> p e j"))
 
         for t in range(-ST, NU + ML + 1):
-            in_u = 0 <= t < NU
-            next_u = 0 <= t + 1 < NU
+            u_leave = t + 1 if t < 1 else t if t > 1 else None
+            in_u = u_leave is not None and 0 <= u_leave < NU
+            u_next = t + 2 if t < 0 else t + 1 if t > 0 else None
+            next_u = u_next is not None and 0 <= u_next < NU
             s_half = half_of(t, ST)
             r_half = half_of(t, RT)
-            n_half = half_of(t, NM)
-            ns_half = half_of(t, NS)
+            n_half = half_of(t, NM) if t > -2 else None
+            ns_half = half_of(t, NS) if t > -1 else None
             g_out, odd_out = divmod(t - ML - 2, 2)
             do_out = odd_out == 0 and 0 <= g_out < NG
 
@@ -268,14 +271,18 @@ def tile_toyattnsublayer_pa_t_kernel(tc, h, ln_w, ln_b, w_q, w_k, w_v, out_0, ou
                         normalise(g, i)
             for j in range(4):
                 if in_u:
-                    leave(t, j)
+                    leave(u_leave, j)
                 if j == 1 and 0 <= g_out < G_OUT:
                     for i in (2 * odd_out, 2 * odd_out + 1):
                         out_copy(g_out, i)
                     if odd_out:
                         store(g_out)
+                if j == 1 and do_out and g_out == NG - 2:
+                    for i in range(GT):
+                        out_copy(g_out, i)
+                    store(g_out)
                 if next_u:
-                    transposes(t + 1, j)
+                    transposes(u_next, j)
             if 0 <= t - ML < NU - 1:
                 quantise(t - ML, slice(0, GTOK))
                 if odd_out:
@@ -301,7 +308,9 @@ def tile_toyattnsublayer_pa_t_kernel(tc, h, ln_w, ln_b, w_q, w_k, w_v, out_0, ou
                     regroup(t - 1, tok)
                 for a in range(2):
                     quantise(t - 1, halves[a])
-            if do_out and g_out >= G_OUT:
+            if do_out and g_out == NG - 2:
+                multiply(t - ML, range(GT))
+            elif do_out and g_out >= G_OUT:
                 for i in range(GT):
                     out_copy(g_out, i)
                 store(g_out)
@@ -318,11 +327,19 @@ def tile_toyattnsublayer_pa_t_kernel(tc, h, ln_w, ln_b, w_q, w_k, w_v, out_0, ou
                 g, tiles = s_half
                 for i in tiles:
                     stats(g, i)
+                    if t == -NM and i == 0:
+                        reciprocal(0, range(GT))
+                        neg_mean_rstd(0, range(GT))
+                        turn_weights(0)
+                        for k in range(GT):
+                            normalise(0, k)
+                        turn_weights(1)
+                        turn_weights(2)
             g_done, odd = divmod(t + 1, 2)
             if odd == 0 and 0 <= g_done < NG - HBUFS:
                 load(g_done + HBUFS)
-            if t == -NS:
-                weights_to_slots()
+            if t == -4:
+                gain_and_bias()
             if t == 0:
                 nc.vector.quantize_mx(
                     out=wcodes[:].rearrange("p c n -> p (c n)").bitcast(FP8X4),

@@ -24,22 +24,39 @@ KP = 512
 NC = D // KP
 NU = NG * NC
 HBUFS = 8
+BN = 512
 
-ST = 5
+ST = 6
 RT = 4
 NM = 3
 NS = 2
-G_OUT = 12
 ML = 2
+EARLY = 1
+CLOSING = 2 * NG - NM
+
+SCALAR_STATS = ((1, 1),)
+STOK = 32
+STOK_UNITS = range(2, 24, 2)
+WARM_UNITS = NU - 4
 
 
-def on_scalar(g, i):
-    return i % 2 == 1
+def normaliser(g, i):
+    if g == 0:
+        return "gpsimd" if i < 2 else "scalar"
+    if g == NG - 1 or (g == NG - 2 and i >= 2):
+        return "vector"
+    if g == 1 or i % 2 == 0 or (i == 1 and in_three(g)):
+        return "gpsimd"
+    return "scalar"
+
+
+def in_three(g):
+    return 1 < g < NG - 2
 
 
 def half_of(t, lead):
     g, r = divmod(t + lead, 2)
-    return (g, (2 * r, 2 * r + 1)) if 0 <= g < NG else None
+    return (g, (2 * r, 2 * r + 1)) if 1 <= g < NG else None
 
 
 def tile_toyattnsublayer_pa_t_kernel(tc, h, ln_w, ln_b, w_q, w_k, w_v, out_0, out_1, out_2):
@@ -55,11 +72,12 @@ def tile_toyattnsublayer_pa_t_kernel(tc, h, ln_w, ln_b, w_q, w_k, w_v, out_0, ou
         plpool = ctx.enter_context(tc.tile_pool(name="plpool", bufs=3))
         grpool = ctx.enter_context(tc.tile_pool(name="grpool", bufs=3))
         cpool = ctx.enter_context(tc.tile_pool(name="cpool", bufs=4))
+        jpool = ctx.enter_context(tc.tile_pool(name="jpool", bufs=2))
         opool = ctx.enter_context(tc.tile_pool(name="opool", bufs=3))
         psum = ctx.enter_context(tc.psum_pool(name="psum", bufs=1))
         ctx.enter_context(tc.manual_schedule())
 
-        hts, sts, mvs, stds, rstds, nmrs, xhs = {}, {}, {}, {}, {}, {}, {}
+        hts, sts, mvs, stds, rstds, negs, xhs, sums = {}, {}, {}, {}, {}, {}, {}, {}
         tps, pls, grs, cds, scs, accs, osts = {}, {}, {}, {}, {}, {}, {}
 
         def load(g, tiles=None):
@@ -78,19 +96,46 @@ def tile_toyattnsublayer_pa_t_kernel(tc, h, ln_w, ln_b, w_q, w_k, w_v, out_0, ou
         def stats(g, i):
             if g not in sts:
                 sts[g] = small.tile([P, GT, 2, 6], F32, name="st")
-            for a in range(2):
-                nc.vector.bn_stats(out=sts[g][:, i, a, :], in_=hts[g][:, i, 512 * a : 512 * (a + 1)])
+            for a in range(D // BN):
+                nc.vector.bn_stats(out=sts[g][:, i, a, :], in_=hts[g][:, i, BN * a : BN * (a + 1)])
 
-        def aggregate(g, i):
+        def mean_and_variance(g):
             if g not in mvs:
                 mvs[g] = small.tile([P, GT, 2], F32, name="mv")
-            nc.vector.bn_aggr(out=mvs[g][:, i, :], in_=sts[g][:, i, :, :].rearrange("p a b -> p (a b)"))
+            return mvs[g]
+
+        def aggregate(g, i):
+            mv = mean_and_variance(g)
+            nc.vector.bn_aggr(out=mv[:, i, :], in_=sts[g][:, i, :, :].rearrange("p a b -> p (a b)"))
+
+        def mean_on_scalar(g, i):
+            mv = mean_and_variance(g)
+            total = small.tile([P, 4], F32, name="total")
+            sums[(g, i)] = total
+            unused = jpool.tile([P, D], BF16, name="unused")
+            nc.scalar.activation(out=unused[:], in_=hts[g][:, i, :], func=ACT.Identity, accum_out=total[:, 0:1])
+            nc.scalar.activation(out=total[:, 1:2], in_=total[:, 0:1], func=ACT.Copy, scale=-1.0 / D)
+            nc.scalar.activation(out=mv[:, i, 0:1], in_=total[:, 0:1], func=ACT.Copy, scale=1.0 / D)
+
+        def variance_on_scalar(g, i):
+            total = sums[(g, i)]
+            unused = jpool.tile([P, D], BF16, name="unused")
+            nc.scalar.activation(
+                out=unused[:],
+                in_=hts[g][:, i, :],
+                func=ACT.Square,
+                bias=total[:, 1:2],
+                accum_out=total[:, 2:3],
+            )
+            nc.scalar.activation(out=mvs[g][:, i, 1:2], in_=total[:, 2:3], func=ACT.Copy, scale=1.0 / D)
 
         def root(g, tiles):
             if g not in stds:
                 stds[g] = small.tile([P, GT], F32, name="std")
+                negs[g] = small.tile([P, GT], F32, name="neg")
             cols = slice(tiles[0], tiles[-1] + 1)
             nc.scalar.activation(out=stds[g][:, cols], in_=mvs[g][:, cols, 1], func=ACT.Sqrt, bias=eps_t[:])
+            nc.scalar.activation(out=negs[g][:, cols], in_=mvs[g][:, cols, 0], func=ACT.Copy, scale=-1.0)
 
         def reciprocal(g, tiles):
             if g not in rstds:
@@ -98,47 +143,42 @@ def tile_toyattnsublayer_pa_t_kernel(tc, h, ln_w, ln_b, w_q, w_k, w_v, out_0, ou
             cols = slice(tiles[0], tiles[-1] + 1)
             nc.vector.reciprocal(rstds[g][:, cols], stds[g][:, cols])
 
-        def neg_mean_rstd(g, tiles):
-            if g not in nmrs:
-                nmrs[g] = small.tile([P, GT], F32, name="nmr")
-            cols = slice(tiles[0], tiles[-1] + 1)
-            nc.vector.scalar_tensor_tensor(
-                out=nmrs[g][:, cols],
-                in0=mvs[g][:, cols, 0],
-                scalar=-1.0,
-                in1=rstds[g][:, cols],
-                op0=ALU.mult,
-                op1=ALU.mult,
-            )
-
-        def normalise(g, i):
+        def normalise(g, i, js=slice(0, 4)):
             if g not in xhs:
                 xhs[g] = xpool.tile([P, GT, 4, D // 4], F32, name="xh")
-            src = hts[g][:, i, :].rearrange("p (b j r) -> p j b r", j=4, r=8)
-            dst = xhs[g][:, i, :, :].rearrange("p j (b r) -> p j b r", r=8)
-            if on_scalar(g, i):
-                nc.scalar.activation(
+            src = hts[g][:, i, :].rearrange("p (b j r) -> p j b r", j=4, r=8)[:, js]
+            dst = xhs[g][:, i, js, :].rearrange("p j (b r) -> p j b r", r=8)
+            engine = normaliser(g, i)
+            rstd = rstds[g][:, i : i + 1]
+            if engine == "vector":
+                nc.vector.tensor_scalar(
                     out=dst,
-                    in_=src,
-                    func=ACT.Identity,
-                    scale=rstds[g][:, i : i + 1],
-                    bias=nmrs[g][:, i : i + 1],
+                    in0=src,
+                    scalar1=mvs[g][:, i, 0:1],
+                    scalar2=rstd,
+                    op0=ALU.subtract,
+                    op1=ALU.mult,
                 )
+            elif engine == "scalar":
+                nmr = small.tile([P, 1], F32, name="nmr")
+                nc.scalar.activation(out=nmr[:], in_=negs[g][:, i : i + 1], func=ACT.Identity, scale=rstd)
+                nc.scalar.activation(out=dst, in_=src, func=ACT.Identity, scale=rstd, bias=nmr[:])
             else:
                 nc.gpsimd.tensor_scalar(
                     out=dst,
                     in0=src,
-                    scalar1=rstds[g][:, i : i + 1],
-                    scalar2=nmrs[g][:, i : i + 1],
-                    op0=ALU.mult,
-                    op1=ALU.add,
+                    scalar1=negs[g][:, i : i + 1],
+                    scalar2=rstd,
+                    op0=ALU.add,
+                    op1=ALU.mult,
                 )
 
         def transposes(u, j):
             g, c = divmod(u, NC)
             tp = psum.tile([P, GTOK], F32, name="tp", tag="T%d" % j)
             tps[(u, j)] = tp
-            nc.tensor.matmul(tp[:, 0:P], lhsT=ident_f[:], rhs=ident_f[:], start=True, stop=True)
+            if u < WARM_UNITS:
+                nc.tensor.matmul(tp[:, 0:P], lhsT=ident_f[:], rhs=ident_f[:], start=True, stop=True)
             for i in range(GT):
                 nc.tensor.transpose(tp[:, P * i : P * (i + 1)], xhs[g][:, i, j, P * c : P * (c + 1)], ident_f[:])
 
@@ -154,13 +194,18 @@ def tile_toyattnsublayer_pa_t_kernel(tc, h, ln_w, ln_b, w_q, w_k, w_v, out_0, ou
                 bias=wb[:, 8 + kb : 9 + kb],
             )
 
-        def regroup(u, tok):
+        def regroup(u, tok, engine):
             if u not in grs:
                 grs[u] = grpool.tile([P, GTOK, 4], BF16, name="gr", align_bytes=64)
-            nc.vector.tensor_copy(
-                out=grs[u][:, tok, :].rearrange("p (c i) t -> p c t i", i=4),
-                in_=pls[u][:, :, tok].rearrange("p t (c i) -> p c t i", i=4),
-            )
+            dst = grs[u][:, tok, :].rearrange("p (c i) j -> p c j i", i=4)
+            src = pls[u][:, :, tok].rearrange("p j (c i) -> p c j i", i=4)
+            if engine == "vector":
+                nc.vector.tensor_copy(out=dst, in_=src)
+            else:
+                nc.scalar.copy(out=dst, in_=src)
+
+        def scalar_tokens(u):
+            return STOK if u in STOK_UNITS else 0
 
         def quantise(u, tok):
             if u not in cds:
@@ -176,7 +221,8 @@ def tile_toyattnsublayer_pa_t_kernel(tc, h, ln_w, ln_b, w_q, w_k, w_v, out_0, ou
             g, c = divmod(u, NC)
             for i in tiles:
                 if c == 0:
-                    accs[(g, i)] = psum.tile([P, 512], F32, name="acc", tag="O%d" % i)
+                    tag = ("T%d" if g == NG - 1 else "O%d") % i
+                    accs[(g, i)] = psum.tile([P, 512], F32, name="acc", tag=tag)
                 nc.tensor.matmul_mx(
                     out=accs[(g, i)][:],
                     lhsT=cds[u][:, P * i : P * (i + 1)].bitcast(FP8X4),
@@ -187,18 +233,19 @@ def tile_toyattnsublayer_pa_t_kernel(tc, h, ln_w, ln_b, w_q, w_k, w_v, out_0, ou
                     stop=(c == NC - 1),
                 )
 
-        def out_copy(g, i):
+        def out_copy(g, i, engine):
             if g not in osts:
                 osts[g] = opool.tile([P, 3, GT, E], F32, name="ost")
             src = accs[(g, i)][:, 0 : 3 * E].rearrange("p (s e) -> p s e", s=3)
-            if i % 2 == 0 if g == NG - 1 else G_OUT <= g < NG - 2:
+            if engine == "vector":
                 nc.vector.tensor_copy(out=osts[g][:, :, i, :], in_=src)
             else:
                 nc.scalar.copy(out=osts[g][:, :, i, :], in_=src)
 
-        def store(g):
+        def store(g, tiles=slice(0, GT)):
+            rows = slice(GT * g + tiles.start, GT * g + tiles.stop)
             for s in range(3):
-                nc.sync.dma_start(out=outs_v[s][:, GT * g : GT * (g + 1), :], in_=osts[g][:, s, :, :])
+                nc.sync.dma_start(out=outs_v[s][:, rows, :], in_=osts[g][:, s, tiles, :])
 
         ident_b = const.tile([P, P], BF16, name="ident_b")
         make_identity(nc, ident_b[:])
@@ -219,31 +266,34 @@ def tile_toyattnsublayer_pa_t_kernel(tc, h, ln_w, ln_b, w_q, w_k, w_v, out_0, ou
                     out=lnrows[8 * r + 4 * c : 8 * r + 4 * (c + 1), :].rearrange("j (b r) -> j b r", r=8),
                     in_=vec[KP * c : KP * (c + 1)].rearrange("(b j r) -> j b r", j=4, r=8),
                 )
+        load(1, range(GT))
         wraw = const.tile([P, 3, D], BF16, name="wraw")
         for s, w in enumerate((w_q, w_k, w_v)):
             nc.sync.dma_start(out=wraw[:, s, :], in_=w)
-        load(1, range(GT))
-        for g in range(2, HBUFS):
+        load(2, range(GT))
+        for g in range(3, HBUFS):
             load(g)
 
-        wslots = const.tile([P, 3, 4, D // 4], BF16, name="wslots")
-        for s in range(3):
-            nc.gpsimd.tensor_scalar(
-                out=wslots[:, s, :, :].rearrange("p j (b r) -> p j b r", r=8),
-                in0=wraw[:, s, :].rearrange("p (b j r) -> p j b r", j=4, r=8),
-                scalar1=1.0,
-                scalar2=0.0,
-                op0=ALU.mult,
-                op1=ALU.add,
-            )
         wb = const.tile([P, 16], F32, name="wb")
         wcodes = const.tile([P, NC, 512], U32, name="wcodes", align_bytes=64)
         wscales = const.tile([P, NC, 512], U8, name="wscales", align_bytes=64)
+        wslots = const.tile([P, 3, 4, D // 4], BF16, name="wslots")
 
         def gain_and_bias():
             ln_ps = psum.tile([P, P], BF16, name="ln_ps", tag="O2")
             nc.tensor.transpose(ln_ps[:], lnrows[:], ident_b[:])
             nc.scalar.copy(out=wb[:], in_=ln_ps[:, 0:16])
+
+        def weights_to_slots():
+            for s in range(3):
+                nc.gpsimd.tensor_scalar(
+                    out=wslots[:, s, :, :].rearrange("p j (b r) -> p j b r", r=8),
+                    in0=wraw[:, s, :].rearrange("p (b j r) -> p j b r", j=4, r=8),
+                    scalar1=1.0,
+                    scalar2=0.0,
+                    op0=ALU.mult,
+                    op1=ALU.add,
+                )
 
         def turn_weights(s):
             for c in range(NC):
@@ -252,97 +302,144 @@ def tile_toyattnsublayer_pa_t_kernel(tc, h, ln_w, ln_b, w_q, w_k, w_v, out_0, ou
                     nc.tensor.transpose(wt[:, j, :], wslots[:, s, j, P * c : P * (c + 1)], ident_b[:])
                 nc.scalar.copy(out=wg[:, c, E * s : E * (s + 1), :], in_=wt[:].rearrange("p j e -> p e j"))
 
-        for t in range(-ST, NU + ML + 1):
-            u_leave = t + 1 if t < 1 else t if t > 1 else None
-            in_u = u_leave is not None and 0 <= u_leave < NU
-            u_next = t + 2 if t < 0 else t + 1 if t > 0 else None
-            next_u = u_next is not None and 0 <= u_next < NU
-            s_half = half_of(t, ST)
-            r_half = half_of(t, RT)
-            n_half = half_of(t, NM) if t > -2 else None
-            ns_half = half_of(t, NS) if t > -1 else None
-            g_out, odd_out = divmod(t - ML - 2, 2)
-            do_out = odd_out == 0 and 0 <= g_out < NG
+        def quantise_weights():
+            nc.vector.quantize_mx(
+                out=wcodes[:].rearrange("p c n -> p (c n)").bitcast(FP8X4),
+                scales=wscales[:].rearrange("p c n -> p (c n)"),
+                in_=wg[:].rearrange("p c n j -> p (c n j)"),
+            )
 
-            if ns_half is not None:
-                g, tiles = ns_half
+        def finish(tiles):
+            reciprocal(0, tiles)
+            for i in tiles:
+                normalise(0, i)
+
+        def statistics(t):
+            half = half_of(t, ST)
+            if half is None:
+                return
+            g, tiles = half
+            mine = [i for i in tiles if (g, i) not in SCALAR_STATS]
+            for i in mine:
+                stats(g, i)
+                if (g, i) == (1, 0):
+                    finish((GT - 1,))
+            for i in mine:
+                aggregate(g, i)
+
+        def norms(t):
+            half = half_of(t, NM)
+            if half is None:
+                return
+            g, tiles = half
+            reciprocal(g, tiles)
+            for i in tiles:
+                if normaliser(g, i) != "scalar" and not (i == 1 and in_three(g)):
+                    normalise(g, i)
+            if in_three(g):
+                normalise(g, 1, slice(tiles[0], tiles[0] + 2))
+
+        def passes(t):
+            if t % 2 == 0:
+                multiply(t - ML, (0, 1))
+            else:
+                multiply(t - ML - 1, (2, 3))
+                multiply(t - ML, range(GT))
+
+        def outs(t, engine):
+            g, odd = divmod(t - ML - 2, 2)
+            if g >= 0:
+                for i in (2 * odd, 2 * odd + 1):
+                    out_copy(g, i, engine)
+                if odd:
+                    store(g)
+
+        for i in range(GT):
+            stats(0, i)
+            aggregate(0, i)
+            root(0, (i,))
+            if i > 0:
+                finish((i - 1,))
+
+        for t in range(2 - ST, EARLY):
+            if t == 2 - ST:
+                gain_and_bias()
+                weights_to_slots()
+            norms(t)
+            g, tiles = half_of(t, ST)
+            for i in tiles:
+                if (g, i) in SCALAR_STATS:
+                    mean_on_scalar(g, i)
+                    variance_on_scalar(g, i)
+            statistics(t)
+            if tiles[-1] == GT - 1:
+                root(g, range(GT))
+            for j in range(4):
+                if t + 2 in (0, 1):
+                    leave(t + 2, j)
+                if t + 3 in (0, 1):
+                    transposes(t + 3, j)
+            if t == -1:
+                turn_weights(0)
+                turn_weights(1)
+                load(HBUFS)
+            if t == 0:
+                turn_weights(2)
+
+        for t in range(EARLY, CLOSING):
+            half = half_of(t, NS)
+            if half is not None:
+                g, tiles = half
                 for i in tiles:
-                    if on_scalar(g, i):
+                    if normaliser(g, i) == "scalar":
                         normalise(g, i)
             for j in range(4):
-                if in_u:
-                    leave(u_leave, j)
-                if j == 1 and 0 <= g_out < G_OUT:
-                    for i in (2 * odd_out, 2 * odd_out + 1):
-                        out_copy(g_out, i)
-                    if odd_out:
-                        store(g_out)
-                if j == 1 and do_out and g_out == NG - 2:
-                    for i in range(GT):
-                        out_copy(g_out, i)
-                    store(g_out)
-                if next_u:
-                    transposes(u_next, j)
-            if 0 <= t - ML < NU - 1:
+                if t > 1:
+                    leave(t, j)
+                if j == 0:
+                    g, odd = divmod(t + RT, 2)
+                    if not odd and 2 < g < NG:
+                        root(g, range(GT))
+                    if scalar_tokens(t - 1):
+                        regroup(t - 1, slice(GTOK - STOK, GTOK), "scalar")
+                if j == 3:
+                    outs(t, "scalar")
+                transposes(t + 1, j)
+            if t >= ML:
                 quantise(t - ML, slice(0, GTOK))
-                if odd_out:
-                    if g_out < G_OUT:
-                        multiply(t - ML - 1, (2, 3))
-                    multiply(t - ML, range(GT))
-                elif g_out < G_OUT:
-                    multiply(t - ML, (0, 1))
-            if n_half is not None:
-                reciprocal(*n_half)
-            if r_half is not None:
-                g, tiles = r_half
-                for i in tiles:
-                    aggregate(g, i)
-                root(g, tiles)
-            if n_half is not None:
-                neg_mean_rstd(*n_half)
-            if 0 <= t - 1 < NU - 1:
-                regroup(t - 1, slice(0, GTOK))
-            if t - 1 == NU - 1:
-                halves = [slice(GTOK // 2 * a, GTOK // 2 * (a + 1)) for a in range(2)]
-                for tok in halves:
-                    regroup(t - 1, tok)
-                for a in range(2):
-                    quantise(t - 1, halves[a])
-            if do_out and g_out == NG - 2:
-                multiply(t - ML, range(GT))
-            elif do_out and g_out >= G_OUT:
-                for i in range(GT):
-                    out_copy(g_out, i)
-                store(g_out)
-                if t - ML < NU:
-                    multiply(t - ML, range(GT))
-            if t - 1 == NU - 1:
-                multiply(t - 1, range(GT))
-            if n_half is not None:
-                g, tiles = n_half
-                for i in tiles:
-                    if not on_scalar(g, i):
-                        normalise(g, i)
-            if s_half is not None:
-                g, tiles = s_half
-                for i in tiles:
-                    stats(g, i)
-                    if t == -NM and i == 0:
-                        reciprocal(0, range(GT))
-                        neg_mean_rstd(0, range(GT))
-                        turn_weights(0)
-                        for k in range(GT):
-                            normalise(0, k)
-                        turn_weights(1)
-                        turn_weights(2)
+            regroup(t - 1, slice(0, GTOK - scalar_tokens(t - 1)), "vector")
+            norms(t)
+            if t >= ML:
+                passes(t)
+            statistics(t)
+            if t == 1:
+                quantise_weights()
             g_done, odd = divmod(t + 1, 2)
-            if odd == 0 and 0 <= g_done < NG - HBUFS:
+            if not odd and g_done < NG - HBUFS:
                 load(g_done + HBUFS)
-            if t == -4:
-                gain_and_bias()
-            if t == 0:
-                nc.vector.quantize_mx(
-                    out=wcodes[:].rearrange("p c n -> p (c n)").bitcast(FP8X4),
-                    scales=wscales[:].rearrange("p c n -> p (c n)"),
-                    in_=wg[:].rearrange("p c n j -> p (c n j)"),
-                )
+
+        for t in range(CLOSING, NU):
+            outs(t, "vector")
+            quantise(t - ML, slice(0, GTOK))
+            passes(t)
+            for j in range(4):
+                leave(t, j)
+                if t + 1 < NU:
+                    transposes(t + 1, j)
+            regroup(t - 1, slice(0, GTOK), "vector")
+
+        for i in range(GT):
+            out_copy(NG - 2, i, "scalar")
+        store(NG - 2)
+        quantise(NU - 2, slice(0, GTOK))
+        multiply(NU - 2, range(GT))
+        halves = (slice(0, GTOK // 2), slice(GTOK // 2, GTOK))
+        for tok in halves:
+            regroup(NU - 1, tok, "vector")
+        for a in range(2):
+            quantise(NU - 1, halves[a])
+            multiply(NU - 1, (2 * a, 2 * a + 1))
+        for i in range(GT):
+            out_copy(NG - 1, i, "vector" if i % 2 == 0 else "scalar")
+            if i % 2 == 1:
+                store(NG - 1, slice(i - 1, i + 1))

from contextlib import ExitStack

import concourse.mybir as mybir
from concourse.masks import make_identity

F32 = mybir.dt.float32
BF16 = mybir.dt.bfloat16
U32 = mybir.dt.uint32
U8 = mybir.dt.uint8
FP8X4 = mybir.dt.float8_e4m3fn_x4
ALU = mybir.AluOpType
ACT = mybir.ActivationFunctionType

T, D, E = 8192, 1024, 128
EPS = 1e-05
FLOPS = 2 * T * D * 3 * E

P = 128
NT = T // P
GT = 4
NG = NT // GT
GTOK = GT * P
KP = 512
NC = D // KP
NU = NG * NC
HBUFS = 8
BN = 512

ST = 6
RT = 4
NM = 3
NS = 2
ML = 2
EARLY = 1
CLOSING = 2 * NG - NM

SCALAR_STATS = ((1, 1),)
STOK = 32
STOK_UNITS = range(2, 24, 2)
WARM_UNITS = NU - 4


def normaliser(g, i):
    if g == 0:
        return "gpsimd" if i < 2 else "scalar"
    if g == NG - 1 or (g == NG - 2 and i >= 2):
        return "vector"
    if g == 1 or i % 2 == 0 or (i == 1 and in_three(g)):
        return "gpsimd"
    return "scalar"


def in_three(g):
    return 1 < g < NG - 2


def half_of(t, lead):
    g, r = divmod(t + lead, 2)
    return (g, (2 * r, 2 * r + 1)) if 1 <= g < NG else None


def tile_toyattnsublayer_pa_t_kernel(tc, h, ln_w, ln_b, w_q, w_k, w_v, out_0, out_1, out_2):
    nc = tc.nc
    h_v = h.rearrange("(p n) k -> p n k", n=NT)
    outs_v = [o.rearrange("(p n) e -> p n e", n=NT) for o in (out_0, out_1, out_2)]

    with ExitStack() as ctx:
        const = ctx.enter_context(tc.tile_pool(name="const", bufs=1))
        hpool = ctx.enter_context(tc.tile_pool(name="hpool", bufs=HBUFS))
        small = ctx.enter_context(tc.tile_pool(name="small", bufs=4))
        xpool = ctx.enter_context(tc.tile_pool(name="xpool", bufs=3))
        plpool = ctx.enter_context(tc.tile_pool(name="plpool", bufs=3))
        grpool = ctx.enter_context(tc.tile_pool(name="grpool", bufs=3))
        cpool = ctx.enter_context(tc.tile_pool(name="cpool", bufs=4))
        jpool = ctx.enter_context(tc.tile_pool(name="jpool", bufs=2))
        opool = ctx.enter_context(tc.tile_pool(name="opool", bufs=3))
        psum = ctx.enter_context(tc.psum_pool(name="psum", bufs=1))
        ctx.enter_context(tc.manual_schedule())

        hts, sts, mvs, stds, rstds, negs, xhs, sums = {}, {}, {}, {}, {}, {}, {}, {}
        tps, pls, grs, cds, scs, accs, osts = {}, {}, {}, {}, {}, {}, {}

        def load(g, tiles=None):
            if g not in hts:
                hts[g] = hpool.tile([P, GT, D], BF16, name="ht")
            ht = hts[g]
            if tiles is None:
                nc.sync.dma_start(out=ht[:], in_=h_v[:, GT * g : GT * (g + 1), :])
            else:
                for i in tiles:
                    n = 2 if (g, i) == (0, 0) else 1
                    for a in range(n):
                        cols = slice(D // n * a, D // n * (a + 1))
                        nc.sync.dma_start(out=ht[:, i, cols], in_=h_v[:, GT * g + i, cols])

        def stats(g, i):
            if g not in sts:
                sts[g] = small.tile([P, GT, 2, 6], F32, name="st")
            for a in range(D // BN):
                nc.vector.bn_stats(out=sts[g][:, i, a, :], in_=hts[g][:, i, BN * a : BN * (a + 1)])

        def mean_and_variance(g):
            if g not in mvs:
                mvs[g] = small.tile([P, GT, 2], F32, name="mv")
            return mvs[g]

        def aggregate(g, i):
            mv = mean_and_variance(g)
            nc.vector.bn_aggr(out=mv[:, i, :], in_=sts[g][:, i, :, :].rearrange("p a b -> p (a b)"))

        def mean_on_scalar(g, i):
            mv = mean_and_variance(g)
            total = small.tile([P, 4], F32, name="total")
            sums[(g, i)] = total
            unused = jpool.tile([P, D], BF16, name="unused")
            nc.scalar.activation(out=unused[:], in_=hts[g][:, i, :], func=ACT.Identity, accum_out=total[:, 0:1])
            nc.scalar.activation(out=total[:, 1:2], in_=total[:, 0:1], func=ACT.Copy, scale=-1.0 / D)
            nc.scalar.activation(out=mv[:, i, 0:1], in_=total[:, 0:1], func=ACT.Copy, scale=1.0 / D)

        def variance_on_scalar(g, i):
            total = sums[(g, i)]
            unused = jpool.tile([P, D], BF16, name="unused")
            nc.scalar.activation(
                out=unused[:],
                in_=hts[g][:, i, :],
                func=ACT.Square,
                bias=total[:, 1:2],
                accum_out=total[:, 2:3],
            )
            nc.scalar.activation(out=mvs[g][:, i, 1:2], in_=total[:, 2:3], func=ACT.Copy, scale=1.0 / D)

        def root(g, tiles):
            if g not in stds:
                stds[g] = small.tile([P, GT], F32, name="std")
                negs[g] = small.tile([P, GT], F32, name="neg")
            cols = slice(tiles[0], tiles[-1] + 1)
            nc.scalar.activation(out=stds[g][:, cols], in_=mvs[g][:, cols, 1], func=ACT.Sqrt, bias=eps_t[:])
            nc.scalar.activation(out=negs[g][:, cols], in_=mvs[g][:, cols, 0], func=ACT.Copy, scale=-1.0)

        def reciprocal(g, tiles):
            if g not in rstds:
                rstds[g] = small.tile([P, GT], F32, name="rstd")
            cols = slice(tiles[0], tiles[-1] + 1)
            nc.vector.reciprocal(rstds[g][:, cols], stds[g][:, cols])

        def normalise(g, i, js=slice(0, 4)):
            if g not in xhs:
                xhs[g] = xpool.tile([P, GT, 4, D // 4], F32, name="xh")
            src = hts[g][:, i, :].rearrange("p (b j r) -> p j b r", j=4, r=8)[:, js]
            dst = xhs[g][:, i, js, :].rearrange("p j (b r) -> p j b r", r=8)
            engine = normaliser(g, i)
            rstd = rstds[g][:, i : i + 1]
            if engine == "vector":
                nc.vector.tensor_scalar(
                    out=dst,
                    in0=src,
                    scalar1=mvs[g][:, i, 0:1],
                    scalar2=rstd,
                    op0=ALU.subtract,
                    op1=ALU.mult,
                )
            elif engine == "scalar":
                nmr = small.tile([P, 1], F32, name="nmr")
                nc.scalar.activation(out=nmr[:], in_=negs[g][:, i : i + 1], func=ACT.Identity, scale=rstd)
                nc.scalar.activation(out=dst, in_=src, func=ACT.Identity, scale=rstd, bias=nmr[:])
            else:
                nc.gpsimd.tensor_scalar(
                    out=dst,
                    in0=src,
                    scalar1=negs[g][:, i : i + 1],
                    scalar2=rstd,
                    op0=ALU.add,
                    op1=ALU.mult,
                )

        def transposes(u, j):
            g, c = divmod(u, NC)
            tp = psum.tile([P, GTOK], F32, name="tp", tag="T%d" % j)
            tps[(u, j)] = tp
            if u < WARM_UNITS:
                nc.tensor.matmul(tp[:, 0:P], lhsT=ident_f[:], rhs=ident_f[:], start=True, stop=True)
            for i in range(GT):
                nc.tensor.transpose(tp[:, P * i : P * (i + 1)], xhs[g][:, i, j, P * c : P * (c + 1)], ident_f[:])

        def leave(u, j):
            kb = 4 * (u % NC) + j
            if u not in pls:
                pls[u] = plpool.tile([P, 4, GTOK], BF16, name="pl")
            nc.scalar.activation(
                out=pls[u][:, j, :],
                in_=tps[(u, j)][:],
                func=ACT.Identity,
                scale=wb[:, kb : kb + 1],
                bias=wb[:, 8 + kb : 9 + kb],
            )

        def regroup(u, tok, engine):
            if u not in grs:
                grs[u] = grpool.tile([P, GTOK, 4], BF16, name="gr", align_bytes=64)
            dst = grs[u][:, tok, :].rearrange("p (c i) j -> p c j i", i=4)
            src = pls[u][:, :, tok].rearrange("p j (c i) -> p c j i", i=4)
            if engine == "vector":
                nc.vector.tensor_copy(out=dst, in_=src)
            else:
                nc.scalar.copy(out=dst, in_=src)

        def scalar_tokens(u):
            return STOK if u in STOK_UNITS else 0

        def quantise(u, tok):
            if u not in cds:
                cds[u] = cpool.tile([P, GTOK], U32, name="codes", align_bytes=64)
                scs[u] = cpool.tile([P, GTOK], U8, name="scl", align_bytes=64)
            nc.vector.quantize_mx(
                out=cds[u][:, tok].bitcast(FP8X4),
                scales=scs[u][:, tok],
                in_=grs[u][:, tok, :].rearrange("p n j -> p (n j)"),
            )

        def multiply(u, tiles):
            g, c = divmod(u, NC)
            for i in tiles:
                if c == 0:
                    tag = ("T%d" if g == NG - 1 else "O%d") % i
                    accs[(g, i)] = psum.tile([P, 512], F32, name="acc", tag=tag)
                nc.tensor.matmul_mx(
                    out=accs[(g, i)][:],
                    lhsT=cds[u][:, P * i : P * (i + 1)].bitcast(FP8X4),
                    lhsT_scale=scs[u][:, P * i : P * (i + 1)],
                    rhs=wcodes[:, c, :].bitcast(FP8X4),
                    rhs_scale=wscales[:, c, :],
                    start=(c == 0),
                    stop=(c == NC - 1),
                )

        def out_copy(g, i, engine):
            if g not in osts:
                osts[g] = opool.tile([P, 3, GT, E], F32, name="ost")
            src = accs[(g, i)][:, 0 : 3 * E].rearrange("p (s e) -> p s e", s=3)
            if engine == "vector":
                nc.vector.tensor_copy(out=osts[g][:, :, i, :], in_=src)
            else:
                nc.scalar.copy(out=osts[g][:, :, i, :], in_=src)

        def store(g, tiles=slice(0, GT)):
            rows = slice(GT * g + tiles.start, GT * g + tiles.stop)
            for s in range(3):
                nc.sync.dma_start(out=outs_v[s][:, rows, :], in_=osts[g][:, s, tiles, :])

        ident_b = const.tile([P, P], BF16, name="ident_b")
        make_identity(nc, ident_b[:])
        ident_f = const.tile([P, P], F32, name="ident_f")
        make_identity(nc, ident_f[:])
        lnrows = const.tile([P, P], BF16, name="lnrows")
        nc.vector.memset(lnrows[:], 0.0)
        eps_t = const.tile([P, 1], F32, name="eps_t")
        nc.vector.memset(eps_t[:], 0.0)
        nc.vector.tensor_scalar(out=eps_t[:], in0=eps_t[:], scalar1=EPS, scalar2=None, op0=ALU.add)
        wg = const.tile([P, NC, 512, 4], BF16, name="wg", align_bytes=64)
        nc.vector.memset(wg[:, :, 3 * E : 512, :], 0.0)

        load(0, range(GT))
        for r, vec in enumerate((ln_w, ln_b)):
            for c in range(NC):
                nc.sync.dma_start(
                    out=lnrows[8 * r + 4 * c : 8 * r + 4 * (c + 1), :].rearrange("j (b r) -> j b r", r=8),
                    in_=vec[KP * c : KP * (c + 1)].rearrange("(b j r) -> j b r", j=4, r=8),
                )
        load(1, range(GT))
        wraw = const.tile([P, 3, D], BF16, name="wraw")
        for s, w in enumerate((w_q, w_k, w_v)):
            nc.sync.dma_start(out=wraw[:, s, :], in_=w)
        load(2, range(GT))
        for g in range(3, HBUFS):
            load(g)

        wb = const.tile([P, 16], F32, name="wb")
        wcodes = const.tile([P, NC, 512], U32, name="wcodes", align_bytes=64)
        wscales = const.tile([P, NC, 512], U8, name="wscales", align_bytes=64)
        wslots = const.tile([P, 3, 4, D // 4], BF16, name="wslots")

        def gain_and_bias():
            ln_ps = psum.tile([P, P], BF16, name="ln_ps", tag="O2")
            nc.tensor.transpose(ln_ps[:], lnrows[:], ident_b[:])
            nc.scalar.copy(out=wb[:], in_=ln_ps[:, 0:16])

        def weights_to_slots():
            for s in range(3):
                nc.gpsimd.tensor_scalar(
                    out=wslots[:, s, :, :].rearrange("p j (b r) -> p j b r", r=8),
                    in0=wraw[:, s, :].rearrange("p (b j r) -> p j b r", j=4, r=8),
                    scalar1=1.0,
                    scalar2=0.0,
                    op0=ALU.mult,
                    op1=ALU.add,
                )

        def turn_weights(s):
            for c in range(NC):
                wt = psum.tile([P, 4, E], BF16, name="wt", tag="O%d" % ((NC * s + c) % GT))
                for j in range(4):
                    nc.tensor.transpose(wt[:, j, :], wslots[:, s, j, P * c : P * (c + 1)], ident_b[:])
                nc.scalar.copy(out=wg[:, c, E * s : E * (s + 1), :], in_=wt[:].rearrange("p j e -> p e j"))

        def quantise_weights():
            nc.vector.quantize_mx(
                out=wcodes[:].rearrange("p c n -> p (c n)").bitcast(FP8X4),
                scales=wscales[:].rearrange("p c n -> p (c n)"),
                in_=wg[:].rearrange("p c n j -> p (c n j)"),
            )

        def finish(tiles):
            reciprocal(0, tiles)
            for i in tiles:
                normalise(0, i)

        def statistics(t):
            half = half_of(t, ST)
            if half is None:
                return
            g, tiles = half
            mine = [i for i in tiles if (g, i) not in SCALAR_STATS]
            for i in mine:
                stats(g, i)
                if (g, i) == (1, 0):
                    finish((GT - 1,))
            for i in mine:
                aggregate(g, i)

        def norms(t):
            half = half_of(t, NM)
            if half is None:
                return
            g, tiles = half
            reciprocal(g, tiles)
            for i in tiles:
                if normaliser(g, i) != "scalar" and not (i == 1 and in_three(g)):
                    normalise(g, i)
            if in_three(g):
                normalise(g, 1, slice(tiles[0], tiles[0] + 2))

        def passes(t):
            if t % 2 == 0:
                multiply(t - ML, (0, 1))
            else:
                multiply(t - ML - 1, (2, 3))
                multiply(t - ML, range(GT))

        def outs(t, engine):
            g, odd = divmod(t - ML - 2, 2)
            if g >= 0:
                for i in (2 * odd, 2 * odd + 1):
                    out_copy(g, i, engine)
                if odd:
                    store(g)

        for i in range(GT):
            stats(0, i)
            aggregate(0, i)
            root(0, (i,))
            if i > 0:
                finish((i - 1,))

        for t in range(2 - ST, EARLY):
            if t == 2 - ST:
                gain_and_bias()
                weights_to_slots()
            norms(t)
            g, tiles = half_of(t, ST)
            for i in tiles:
                if (g, i) in SCALAR_STATS:
                    mean_on_scalar(g, i)
                    variance_on_scalar(g, i)
            statistics(t)
            if tiles[-1] == GT - 1:
                root(g, range(GT))
            for j in range(4):
                if t + 2 in (0, 1):
                    leave(t + 2, j)
                if t + 3 in (0, 1):
                    transposes(t + 3, j)
            if t == -1:
                turn_weights(0)
                turn_weights(1)
                load(HBUFS)
            if t == 0:
                turn_weights(2)

        for t in range(EARLY, CLOSING):
            half = half_of(t, NS)
            if half is not None:
                g, tiles = half
                for i in tiles:
                    if normaliser(g, i) == "scalar":
                        normalise(g, i)
            for j in range(4):
                if t > 1:
                    leave(t, j)
                if j == 0:
                    g, odd = divmod(t + RT, 2)
                    if not odd and 2 < g < NG:
                        root(g, range(GT))
                    if scalar_tokens(t - 1):
                        regroup(t - 1, slice(GTOK - STOK, GTOK), "scalar")
                if j == 3:
                    outs(t, "scalar")
                transposes(t + 1, j)
            if t >= ML:
                quantise(t - ML, slice(0, GTOK))
            regroup(t - 1, slice(0, GTOK - scalar_tokens(t - 1)), "vector")
            norms(t)
            if t >= ML:
                passes(t)
            statistics(t)
            if t == 1:
                quantise_weights()
            g_done, odd = divmod(t + 1, 2)
            if not odd and g_done < NG - HBUFS:
                load(g_done + HBUFS)

        for t in range(CLOSING, NU):
            outs(t, "vector")
            quantise(t - ML, slice(0, GTOK))
            passes(t)
            for j in range(4):
                leave(t, j)
                if t + 1 < NU:
                    transposes(t + 1, j)
            regroup(t - 1, slice(0, GTOK), "vector")

        for i in range(GT):
            out_copy(NG - 2, i, "scalar")
        store(NG - 2)
        quantise(NU - 2, slice(0, GTOK))
        multiply(NU - 2, range(GT))
        halves = (slice(0, GTOK // 2), slice(GTOK // 2, GTOK))
        for tok in halves:
            regroup(NU - 1, tok, "vector")
        for a in range(2):
            quantise(NU - 1, halves[a])
            multiply(NU - 1, (2 * a, 2 * a + 1))
        for i in range(GT):
            out_copy(NG - 1, i, "vector" if i % 2 == 0 else "scalar")
            if i % 2 == 1:
                store(NG - 1, slice(i - 1, i + 1))
